import numpy as np
import ml_dtypes


def mxq(x, axis, fmt="e4m3"):
    dtype, down = {"e4m3": (ml_dtypes.float8_e4m3fn, 7), "e5m2": (ml_dtypes.float8_e5m2, 14)}[fmt]
    v = np.moveaxis(np.asarray(x, np.float32).astype(ml_dtypes.bfloat16).astype(np.float64), axis, -1)
    blocks = v.reshape(v.shape[:-1] + (-1, 32))
    amax = np.abs(blocks).max(-1, keepdims=True)
    byte = np.maximum(np.where(amax > 0, np.frexp(amax)[1] - 1 + 127, 0) - down, 1)
    scale = np.exp2(byte - 127.0)
    codes = (blocks / scale).astype(np.float32).astype(dtype).astype(np.float64)
    return np.moveaxis((codes * scale).reshape(v.shape), -1, axis)


WIDE = False


def mx_kscale(k):
    if not WIDE:
        return np.ones(k)
    levels = np.array([10, -10, 5, -5, 0])
    if k % 512:
        return np.exp2(np.random.permutation(np.resize(levels, k // 32))).repeat(32)
    a = np.empty((k // 512, 16))
    for p in range(k // 512):
        a[p, :8] = np.random.permutation(np.resize(levels, 8))
        for g in range(8):
            far = levels[np.abs(levels - a[p, g]) >= 10]
            a[p, g + 8] = far[np.random.randint(len(far))]
    return np.exp2(a.ravel()).repeat(32)


BF16 = ml_dtypes.bfloat16


def bf(x):
    return np.asarray(x, np.float32).astype(BF16)


def f64(x):
    return np.asarray(x).astype(np.float64)


B, T, DIM, H, D = 16, 1024, 128, 4, 128
E = H * D


def softmax(z):
    e = np.exp(z - z.max(-1, keepdims=True))
    return e / e.sum(-1, keepdims=True)


def setup_inputs():
    u = mx_kscale(E).reshape(H, D)
    q = softmax(3.0 * np.random.standard_normal((B, H, T, D)))
    k_sum = (T / D) * np.exp(0.3 * np.random.standard_normal((B, H, 1, D)))
    amp = 2.0 * np.sqrt(T * np.mean(q * q))
    context = k_sum.transpose(0, 1, 3, 2) * 0.2 * np.random.standard_normal((1, H, 1, D)) + amp * np.random.standard_normal((B, H, D, D))
    return {"q": bf(q * u[None, :, None, :]),
            "k_sum": bf(k_sum / u[None, :, None, :]),
            "context": bf(context * u[None, :, None, :] / u[None, :, :, None]),
            "Wp": bf(np.random.standard_normal((DIM, E)) * 2.0 / np.sqrt(E) / u.reshape(E)),
            "bp": bf(np.random.standard_normal(DIM) * 0.2)}


def reference(q, k_sum, context, Wp, bp):
    d_inv = 1.0 / (f64(q) * f64(k_sum)).sum(axis=-1, keepdims=True)
    o = (f64(q) @ f64(context)) * d_inv + f64(q)
    o = o.transpose(0, 2, 1, 3).reshape(B, T, E)
    return (mxq(o, 2, "e4m3") @ mxq(f64(Wp), 1, "e4m3").T) + f64(bp)

@@ -1,0 +1,264 @@
+from contextlib import ExitStack
+
+import concourse.mybir as mybir
+from concourse.masks import make_identity
+
+BF16 = mybir.dt.bfloat16
+F32 = mybir.dt.float32
+U32 = mybir.dt.uint32
+U8 = mybir.dt.uint8
+FP8X4 = mybir.dt.float8_e4m3fn_x4
+IDENTITY = mybir.ActivationFunctionType.Identity
+MULT = mybir.AluOpType.mult
+ADD = mybir.AluOpType.add
+
+B, H, T, D = 16, 4, 1024, 128
+DIM = 128
+E = H * D
+P = 128
+PACK = 4
+WORD_BLOCKS = 2
+CHUNKS = T // P
+PAIR = 2
+HALF = CHUNKS // 2
+PAIRS_PER_BATCH = CHUNKS // PAIR
+PAIRS_PER_HALF = HALF // PAIR
+HALVES = 2 * B
+PAIRS = B * PAIRS_PER_BATCH
+BIAS_ROW = B * H
+PSUM_BANKS = 8
+
+TRANSPOSE_LEAD = 2
+QUANTISE_LAG = 3
+PROJECT_LAG = 5
+STORE_LAG = 6
+
+QT_BUFS = 4
+DINV_BUFS = 4
+OM_BUFS = 4
+GROUPED_BUFS = 3
+MX_BUFS = 3
+REST_BUFS = 3
+OUT_BUFS = 16
+
+FLOPS = 2 * B * H * T * D * D + 2 * B * T * E * DIM
+
+
+def half_batch_due(r, lag):
+    first_round = r - lag
+    if first_round % PAIRS_PER_HALF == 0 and 0 <= first_round < PAIRS:
+        return first_round // PAIRS_PER_HALF
+    return None
+
+
+def tile_linearattention_pb_t_kernel(tc, q, k_sum, context, Wp, bp, out):
+    nc = tc.nc
+    with ExitStack() as stack:
+        consts = stack.enter_context(tc.tile_pool(name="consts", bufs=1))
+        q_pool = stack.enter_context(tc.tile_pool(name="q", bufs=HALVES))
+        qT_pool = stack.enter_context(tc.tile_pool(name="qT", bufs=QT_BUFS))
+        dinv_pool = stack.enter_context(tc.tile_pool(name="dinv", bufs=DINV_BUFS))
+        om_pool = stack.enter_context(tc.tile_pool(name="om", bufs=OM_BUFS))
+        grouped_pool = stack.enter_context(tc.tile_pool(name="grouped", bufs=GROUPED_BUFS))
+        mx_pool = stack.enter_context(tc.tile_pool(name="mx", bufs=MX_BUFS))
+        resT_pool = stack.enter_context(tc.tile_pool(name="resT", bufs=REST_BUFS))
+        out_pool = stack.enter_context(tc.tile_pool(name="out", bufs=OUT_BUFS))
+        psum = stack.enter_context(tc.psum_pool(name="psum", bufs=PSUM_BANKS))
+        stack.enter_context(tc.manual_schedule())
+
+        small_rows = consts.tile([P, D], BF16)
+        nc.vector.memset(small_rows[:], 0.0)
+        nc.sync.dma_start(out=small_rows[0:BIAS_ROW, :], in_=k_sum.rearrange("b h o d -> (b h o) d"))
+        nc.sync.dma_start(out=small_rows[BIAS_ROW : BIAS_ROW + 1, :], in_=bp.rearrange("(o n) -> o n", o=1))
+        wp_rows = consts.tile([P, E], BF16)
+        ctx = consts.tile([P, B * H, D], BF16)
+        q_tiles = []
+        context_by_feature = context.rearrange("b h d e -> d (b h) e")
+        for b in range(B):
+            q_by_token = q[b].rearrange("h (p c) d -> p h c d", c=CHUNKS)
+            for half in range(2):
+                q_half = q_pool.tile([P, H, HALF, D], BF16)
+                nc.sync.dma_start(out=q_half[:], in_=q_by_token[:, :, half * HALF : (half + 1) * HALF, :])
+                q_tiles.append(q_half)
+                if half == 0:
+                    heads = slice(b * H, (b + 1) * H)
+                    nc.sync.dma_start(out=ctx[:, heads, :], in_=context_by_feature[:, heads, :])
+            if b == 0:
+                nc.sync.dma_start(out=wp_rows[:], in_=Wp)
+
+        ident_bf16 = consts.tile([P, P], BF16)
+        make_identity(nc, ident_bf16[:])
+        ident_f32 = consts.tile([P, P], F32)
+        make_identity(nc, ident_f32[:])
+
+        small_ps = psum.tile([P, P], BF16, tag="bank")
+        nc.tensor.transpose(small_ps[:], small_rows[:], ident_bf16[:])
+        ksumT = consts.tile([P, B * H], BF16)
+        nc.vector.tensor_copy(out=ksumT[:], in_=small_ps[:, 0:BIAS_ROW])
+        bias = consts.tile([P, 1], F32)
+        nc.vector.tensor_copy(out=bias[:], in_=small_ps[:, BIAS_ROW : BIAS_ROW + 1])
+
+        tq_tiles = {}
+        qT_tiles = {}
+        dinv_tiles = {}
+        om_tiles = {}
+        grouped_tiles = {}
+        mx_tiles = {}
+        resT_tiles = {}
+
+        def chunk_in_half(pair, cc):
+            return PAIR * (pair % PAIRS_PER_HALF) + cc
+
+        def transpose_queries(pair, cc):
+            if cc == 0:
+                tq_new = psum.tile([P, PAIR, H, P], BF16, tag="bank")
+                tq_tiles[pair] = tq_new
+            tq = tq_tiles[pair]
+            for h in range(H):
+                nc.tensor.transpose(
+                    tq[:, cc, h, :], q_tiles[pair // PAIRS_PER_HALF][:, h, chunk_in_half(pair, cc), :], ident_bf16[:]
+                )
+            if cc == PAIR - 1:
+                qT = qT_pool.tile([P, PAIR, H, P], BF16)
+                nc.scalar.copy(out=qT[:], in_=tq[:])
+                qT_tiles[pair] = qT
+
+        def denominators(pair):
+            b = pair // PAIRS_PER_BATCH
+            den = psum.tile([P, PAIR, H], F32, tag="bank")
+            for cc in range(PAIR):
+                for h in range(H):
+                    nc.tensor.matmul(
+                        out=den[:, cc, h : h + 1],
+                        lhsT=qT_tiles[pair][:, cc, h, :],
+                        rhs=ksumT[:, b * H + h : b * H + h + 1],
+                        start=True,
+                        stop=True,
+                    )
+            d_inv = dinv_pool.tile([P, PAIR, H], F32)
+            nc.vector.reciprocal(out=d_inv[:], in_=den[:])
+            dinv_tiles[pair] = d_inv
+
+        def multiply(pair, cc):
+            b = pair // PAIRS_PER_BATCH
+            prod = psum.tile([P, H, D], F32, tag="bank")
+            for h in range(H):
+                nc.tensor.matmul(
+                    out=prod[:, h, :], lhsT=qT_tiles[pair][:, cc, h, :], rhs=ctx[:, b * H + h, :], start=True, stop=True
+                )
+            return prod
+
+        def normalise(pair, cc, prod):
+            if cc == 0:
+                om_new = om_pool.tile([P, PAIR, E], BF16)
+                om_tiles[pair] = om_new
+            om_split = om_tiles[pair][:, cc, :].rearrange("p (u f) -> p u f", u=WORD_BLOCKS)
+            for h in range(H):
+                nc.vector.scalar_tensor_tensor(
+                    out=om_split[:, :, h * D // 2 : (h + 1) * D // 2],
+                    in0=prod[:, h, :].rearrange("p (f u) -> p u f", u=WORD_BLOCKS),
+                    scalar=dinv_tiles[pair][:, cc, h : h + 1],
+                    in1=q_tiles[pair // PAIRS_PER_HALF][:, h, chunk_in_half(pair, cc), :].rearrange(
+                        "p (f u) -> p u f", u=WORD_BLOCKS
+                    ),
+                    op0=MULT,
+                    op1=ADD,
+                )
+
+        def transpose_outputs(pair):
+            om_words = om_tiles[pair][:].bitcast(F32)
+            tom = psum.tile([P, PAIR, WORD_BLOCKS, P], F32, tag="bank")
+            for cc in range(PAIR):
+                for u in range(WORD_BLOCKS):
+                    nc.tensor.transpose(tom[:, cc, u, :], om_words[:, cc, u * P : (u + 1) * P], ident_f32[:])
+            if pair % PAIRS_PER_HALF == 0:
+                grouped_new = grouped_pool.tile([P, HALF * P * PACK], BF16, align_bytes=64)
+                grouped_tiles[pair // PAIRS_PER_HALF] = grouped_new
+            grouped_words = (
+                grouped_tiles[pair // PAIRS_PER_HALF][:]
+                .bitcast(F32)
+                .rearrange("p (c t u) -> p c t u", c=HALF, u=WORD_BLOCKS)
+            )
+            first = chunk_in_half(pair, 0)
+            nc.scalar.copy(out=grouped_words[:, first : first + PAIR, :, :], in_=tom[:].rearrange("p c u t -> p c t u"))
+
+        def quantise(half_batch):
+            codes = mx_pool.tile([P, HALF * P], U32, align_bytes=64)
+            scales = mx_pool.tile([P, HALF * P], U8, align_bytes=64)
+            nc.vector.quantize_mx(out=codes[:].bitcast(FP8X4), scales=scales[:], in_=grouped_tiles[half_batch][:])
+            mx_tiles[half_batch] = (codes, scales)
+
+        def project(half_batch):
+            codes, scales = mx_tiles[half_batch]
+            resT = psum.tile([P, HALF * P], F32, tag="bank")
+            nc.tensor.matmul_mx(
+                out=resT[:],
+                lhsT=wp_codes[:].bitcast(FP8X4),
+                lhsT_scale=wp_scales[:],
+                rhs=codes[:].bitcast(FP8X4),
+                rhs_scale=scales[:],
+                start=True,
+                stop=True,
+            )
+            resT_sb = resT_pool.tile([P, HALF * P], F32)
+            nc.scalar.activation(out=resT_sb[:], in_=resT[:], func=IDENTITY, bias=bias[:, 0:1], scale=1.0)
+            resT_tiles[half_batch] = resT_sb
+
+        def store(half_batch):
+            res = psum.tile([P, HALF, DIM], F32, tag="bank")
+            for c in range(HALF):
+                nc.tensor.transpose(res[:, c, :], resT_tiles[half_batch][:, c * P : (c + 1) * P], ident_f32[:])
+            out_sb = out_pool.tile([P, HALF, DIM], F32)
+            nc.scalar.copy(out=out_sb[:], in_=res[:])
+            b, half = divmod(half_batch, 2)
+            out_by_token = out[b].rearrange("(p c) n -> p c n", c=CHUNKS)
+            nc.sync.dma_start(out=out_by_token[:, half * HALF : (half + 1) * HALF, :], in_=out_sb[:])
+
+        def run_round(r):
+            if r < PAIRS:
+                normalise(r, 0, multiply(r, 0))
+            if r + TRANSPOSE_LEAD < PAIRS:
+                transpose_queries(r + TRANSPOSE_LEAD, 0)
+            if half_batch_due(r, PROJECT_LAG) is not None:
+                project(half_batch_due(r, PROJECT_LAG))
+            if half_batch_due(r, STORE_LAG) is not None:
+                store(half_batch_due(r, STORE_LAG))
+            prod = multiply(r, 1) if r < PAIRS else None
+            if r + TRANSPOSE_LEAD < PAIRS:
+                transpose_queries(r + TRANSPOSE_LEAD, 1)
+            if r + 1 < PAIRS:
+                denominators(r + 1)
+            if r < PAIRS:
+                normalise(r, 1, prod)
+            if 0 <= r - 1 < PAIRS:
+                transpose_outputs(r - 1)
+            if half_batch_due(r, QUANTISE_LAG) is not None:
+                quantise(half_batch_due(r, QUANTISE_LAG))
+
+        for pair in range(TRANSPOSE_LEAD):
+            for cc in range(PAIR):
+                transpose_queries(pair, cc)
+        denominators(0)
+        for r in range(2):
+            run_round(r)
+
+        wp_ps = psum.tile([P, WORD_BLOCKS, P], F32, tag="bank")
+        wp_split = consts.tile([P, E], BF16)
+        nc.vector.tensor_copy(
+            out=wp_split[:].rearrange("p (u f) -> p u f", u=WORD_BLOCKS),
+            in_=wp_rows[:].rearrange("p (f u) -> p u f", u=WORD_BLOCKS),
+        )
+        wp_words = wp_split[:].bitcast(F32)
+        for u in range(WORD_BLOCKS):
+            nc.tensor.transpose(wp_ps[:, u, :], wp_words[:, u * P : (u + 1) * P], ident_f32[:])
+        wp_grouped = consts.tile([P, DIM * PACK], BF16, align_bytes=64)
+        nc.vector.tensor_copy(
+            out=wp_grouped[:].bitcast(F32).rearrange("p (n u) -> p n u", u=WORD_BLOCKS),
+            in_=wp_ps[:].rearrange("p u n -> p n u"),
+        )
+        wp_codes = consts.tile([P, DIM], U32, align_bytes=64)
+        wp_scales = consts.tile([P, DIM], U8, align_bytes=64)
+        nc.vector.quantize_mx(out=wp_codes[:].bitcast(FP8X4), scales=wp_scales[:], in_=wp_grouped[:])
+
+        for r in range(2, PAIRS - PAIRS_PER_HALF + STORE_LAG + 1):
+            run_round(r)

@@ -8,7 +8,7 @@ F32 = mybir.dt.float32
 U32 = mybir.dt.uint32
 U8 = mybir.dt.uint8
 FP8X4 = mybir.dt.float8_e4m3fn_x4
-IDENTITY = mybir.ActivationFunctionType.Identity
+COPY = mybir.ActivationFunctionType.Copy
 MULT = mybir.AluOpType.mult
 ADD = mybir.AluOpType.add
 
@@ -28,17 +28,20 @@ PAIRS = B * PAIRS_PER_BATCH
 BIAS_ROW = B * H
 PSUM_BANKS = 8
 
+VECTOR_HEADS = (1, 2)
+
 TRANSPOSE_LEAD = 2
-QUANTISE_LAG = 3
-PROJECT_LAG = 5
-STORE_LAG = 6
+OM_LAG = 2
+QUANTISE_LAG = OM_LAG + 2
+PROJECT_LAG = OM_LAG + 3
+STORE_LAG = OM_LAG + 4
 
 QT_BUFS = 4
 DINV_BUFS = 4
-OM_BUFS = 4
+SCALED_BUFS = 4
+OM_BUFS = 5
 GROUPED_BUFS = 3
 MX_BUFS = 3
-REST_BUFS = 3
 OUT_BUFS = 16
 
 FLOPS = 2 * B * H * T * D * D + 2 * B * T * E * DIM
@@ -58,10 +61,10 @@ def tile_linearattention_pb_t_kernel(tc, q, k_sum, context, Wp, bp, out):
         q_pool = stack.enter_context(tc.tile_pool(name="q", bufs=HALVES))
         qT_pool = stack.enter_context(tc.tile_pool(name="qT", bufs=QT_BUFS))
         dinv_pool = stack.enter_context(tc.tile_pool(name="dinv", bufs=DINV_BUFS))
+        scaled_pool = stack.enter_context(tc.tile_pool(name="scaled", bufs=SCALED_BUFS))
         om_pool = stack.enter_context(tc.tile_pool(name="om", bufs=OM_BUFS))
         grouped_pool = stack.enter_context(tc.tile_pool(name="grouped", bufs=GROUPED_BUFS))
         mx_pool = stack.enter_context(tc.tile_pool(name="mx", bufs=MX_BUFS))
-        resT_pool = stack.enter_context(tc.tile_pool(name="resT", bufs=REST_BUFS))
         out_pool = stack.enter_context(tc.tile_pool(name="out", bufs=OUT_BUFS))
         psum = stack.enter_context(tc.psum_pool(name="psum", bufs=PSUM_BANKS))
         stack.enter_context(tc.manual_schedule())
@@ -95,33 +98,53 @@ def tile_linearattention_pb_t_kernel(tc, q, k_sum, context, Wp, bp, out):
         nc.tensor.transpose(small_ps[:], small_rows[:], ident_bf16[:])
         ksumT = consts.tile([P, B * H], BF16)
         nc.vector.tensor_copy(out=ksumT[:], in_=small_ps[:, 0:BIAS_ROW])
-        bias = consts.tile([P, 1], F32)
-        nc.vector.tensor_copy(out=bias[:], in_=small_ps[:, BIAS_ROW : BIAS_ROW + 1])
+        bias_ps = psum.tile([P, DIM], F32, tag="bank")
+        nc.tensor.matmul(
+            out=bias_ps[:],
+            lhsT=ident_bf16[:, BIAS_ROW : BIAS_ROW + 1].to_broadcast([P, P]),
+            rhs=small_rows[:],
+            start=True,
+            stop=True,
+        )
+        bias = consts.tile([P, HALF, DIM], F32)
+        for c in range(HALF):
+            nc.vector.tensor_copy(out=bias[:, c, :], in_=bias_ps[:])
 
         tq_tiles = {}
         qT_tiles = {}
+        den_tiles = {}
         dinv_tiles = {}
+        product_tiles = {}
         om_tiles = {}
+        tom_tiles = {}
         grouped_tiles = {}
         mx_tiles = {}
-        resT_tiles = {}
+        res_tiles = {}
 
         def chunk_in_half(pair, cc):
             return PAIR * (pair % PAIRS_PER_HALF) + cc
+
+        def split_words(ap):
+            return ap.rearrange("p (f u) -> p u f", u=WORD_BLOCKS)
+
+        def vector_heads(pair, cc):
+            return H if cc == 0 else VECTOR_HEADS[pair % 2]
 
         def transpose_queries(pair, cc):
             if cc == 0:
                 tq_new = psum.tile([P, PAIR, H, P], BF16, tag="bank")
                 tq_tiles[pair] = tq_new
-            tq = tq_tiles[pair]
             for h in range(H):
                 nc.tensor.transpose(
-                    tq[:, cc, h, :], q_tiles[pair // PAIRS_PER_HALF][:, h, chunk_in_half(pair, cc), :], ident_bf16[:]
+                    tq_tiles[pair][:, cc, h, :],
+                    q_tiles[pair // PAIRS_PER_HALF][:, h, chunk_in_half(pair, cc), :],
+                    ident_bf16[:],
                 )
-            if cc == PAIR - 1:
-                qT = qT_pool.tile([P, PAIR, H, P], BF16)
-                nc.scalar.copy(out=qT[:], in_=tq[:])
-                qT_tiles[pair] = qT
+
+        def keep_queries(pair):
+            qT = qT_pool.tile([P, PAIR, H, P], BF16)
+            nc.scalar.copy(out=qT[:], in_=tq_tiles[pair][:])
+            qT_tiles[pair] = qT
 
         def denominators(pair):
             b = pair // PAIRS_PER_BATCH
@@ -135,35 +158,52 @@ def tile_linearattention_pb_t_kernel(tc, q, k_sum, context, Wp, bp, out):
                         start=True,
                         stop=True,
                     )
+            den_tiles[pair] = den
+
+        def invert(pair):
             d_inv = dinv_pool.tile([P, PAIR, H], F32)
-            nc.vector.reciprocal(out=d_inv[:], in_=den[:])
+            nc.vector.reciprocal(out=d_inv[:], in_=den_tiles[pair][:])
             dinv_tiles[pair] = d_inv
 
         def multiply(pair, cc):
             b = pair // PAIRS_PER_BATCH
-            prod = psum.tile([P, H, D], F32, tag="bank")
-            for h in range(H):
-                nc.tensor.matmul(
-                    out=prod[:, h, :], lhsT=qT_tiles[pair][:, cc, h, :], rhs=ctx[:, b * H + h, :], start=True, stop=True
-                )
-            return prod
+            for heads in (range(vector_heads(pair, cc)), range(vector_heads(pair, cc), H)):
+                if len(heads) == 0:
+                    continue
+                product = psum.tile([P, H, D], F32, tag="bank")
+                for h in heads:
+                    nc.tensor.matmul(
+                        out=product[:, h, :],
+                        lhsT=qT_tiles[pair][:, cc, h, :],
+                        rhs=ctx[:, b * H + h, :],
+                        start=True,
+                        stop=True,
+                    )
+                    product_tiles[pair, cc, h] = product
 
-        def normalise(pair, cc, prod):
-            if cc == 0:
+        def om_parts(pair, cc, h):
+            if pair not in om_tiles:
                 om_new = om_pool.tile([P, PAIR, E], BF16)
                 om_tiles[pair] = om_new
             om_split = om_tiles[pair][:, cc, :].rearrange("p (u f) -> p u f", u=WORD_BLOCKS)
-            for h in range(H):
-                nc.vector.scalar_tensor_tensor(
-                    out=om_split[:, :, h * D // 2 : (h + 1) * D // 2],
-                    in0=prod[:, h, :].rearrange("p (f u) -> p u f", u=WORD_BLOCKS),
-                    scalar=dinv_tiles[pair][:, cc, h : h + 1],
-                    in1=q_tiles[pair // PAIRS_PER_HALF][:, h, chunk_in_half(pair, cc), :].rearrange(
-                        "p (f u) -> p u f", u=WORD_BLOCKS
-                    ),
-                    op0=MULT,
-                    op1=ADD,
-                )
+            return (
+                om_split[:, :, h * D // WORD_BLOCKS : (h + 1) * D // WORD_BLOCKS],
+                split_words(product_tiles[pair, cc, h][:, h, :]),
+                dinv_tiles[pair][:, cc, h : h + 1],
+                split_words(q_tiles[pair // PAIRS_PER_HALF][:, h, chunk_in_half(pair, cc), :]),
+            )
+
+        def normalise_vector(pair, cc):
+            for h in range(vector_heads(pair, cc)):
+                om_out, product, d_inv, q_in = om_parts(pair, cc, h)
+                nc.vector.scalar_tensor_tensor(out=om_out, in0=product, scalar=d_inv, in1=q_in, op0=MULT, op1=ADD)
+
+        def normalise_scalar(pair):
+            for h in range(vector_heads(pair, 1), H):
+                om_out, product, d_inv, q_in = om_parts(pair, 1, h)
+                scaled = scaled_pool.tile([P, WORD_BLOCKS, D // WORD_BLOCKS], F32)
+                nc.scalar.activation(out=scaled[:], in_=product, func=COPY, scale=d_inv)
+                nc.gpsimd.tensor_tensor(out=om_out, in0=scaled[:], in1=q_in, op=ADD)
 
         def transpose_outputs(pair):
             om_words = om_tiles[pair][:].bitcast(F32)
@@ -171,6 +211,9 @@ def tile_linearattention_pb_t_kernel(tc, q, k_sum, context, Wp, bp, out):
             for cc in range(PAIR):
                 for u in range(WORD_BLOCKS):
                     nc.tensor.transpose(tom[:, cc, u, :], om_words[:, cc, u * P : (u + 1) * P], ident_f32[:])
+            tom_tiles[pair] = tom
+
+        def regroup(pair):
             if pair % PAIRS_PER_HALF == 0:
                 grouped_new = grouped_pool.tile([P, HALF * P * PACK], BF16, align_bytes=64)
                 grouped_tiles[pair // PAIRS_PER_HALF] = grouped_new
@@ -180,7 +223,9 @@ def tile_linearattention_pb_t_kernel(tc, q, k_sum, context, Wp, bp, out):
                 .rearrange("p (c t u) -> p c t u", c=HALF, u=WORD_BLOCKS)
             )
             first = chunk_in_half(pair, 0)
-            nc.scalar.copy(out=grouped_words[:, first : first + PAIR, :, :], in_=tom[:].rearrange("p c u t -> p c t u"))
+            nc.scalar.copy(
+                out=grouped_words[:, first : first + PAIR, :, :], in_=tom_tiles[pair][:].rearrange("p c u t -> p c t u")
+            )
 
         def quantise(half_batch):
             codes = mx_pool.tile([P, HALF * P], U32, align_bytes=64)
@@ -190,64 +235,74 @@ def tile_linearattention_pb_t_kernel(tc, q, k_sum, context, Wp, bp, out):
 
         def project(half_batch):
             codes, scales = mx_tiles[half_batch]
-            resT = psum.tile([P, HALF * P], F32, tag="bank")
-            nc.tensor.matmul_mx(
-                out=resT[:],
-                lhsT=wp_codes[:].bitcast(FP8X4),
-                lhsT_scale=wp_scales[:],
-                rhs=codes[:].bitcast(FP8X4),
-                rhs_scale=scales[:],
-                start=True,
-                stop=True,
-            )
-            resT_sb = resT_pool.tile([P, HALF * P], F32)
-            nc.scalar.activation(out=resT_sb[:], in_=resT[:], func=IDENTITY, bias=bias[:, 0:1], scale=1.0)
-            resT_tiles[half_batch] = resT_sb
-
-        def store(half_batch):
             res = psum.tile([P, HALF, DIM], F32, tag="bank")
             for c in range(HALF):
-                nc.tensor.transpose(res[:, c, :], resT_tiles[half_batch][:, c * P : (c + 1) * P], ident_f32[:])
+                tokens = slice(c * P, (c + 1) * P)
+                nc.tensor.matmul_mx(
+                    out=res[:, c, :],
+                    lhsT=codes[:, tokens].bitcast(FP8X4),
+                    lhsT_scale=scales[:, tokens],
+                    rhs=wp_codes[:].bitcast(FP8X4),
+                    rhs_scale=wp_scales[:],
+                    start=True,
+                    stop=True,
+                )
+            res_tiles[half_batch] = res
+
+        def store(half_batch):
             out_sb = out_pool.tile([P, HALF, DIM], F32)
-            nc.scalar.copy(out=out_sb[:], in_=res[:])
+            nc.vector.tensor_tensor(out=out_sb[:], in0=res_tiles[half_batch][:], in1=bias[:], op=ADD)
             b, half = divmod(half_batch, 2)
             out_by_token = out[b].rearrange("(p c) n -> p c n", c=CHUNKS)
             nc.sync.dma_start(out=out_by_token[:, half * HALF : (half + 1) * HALF, :], in_=out_sb[:])
 
         def run_round(r):
             if r < PAIRS:
-                normalise(r, 0, multiply(r, 0))
+                multiply(r, 0)
             if r + TRANSPOSE_LEAD < PAIRS:
                 transpose_queries(r + TRANSPOSE_LEAD, 0)
             if half_batch_due(r, PROJECT_LAG) is not None:
                 project(half_batch_due(r, PROJECT_LAG))
-            if half_batch_due(r, STORE_LAG) is not None:
-                store(half_batch_due(r, STORE_LAG))
-            prod = multiply(r, 1) if r < PAIRS else None
+            if r < PAIRS:
+                multiply(r, 1)
             if r + TRANSPOSE_LEAD < PAIRS:
                 transpose_queries(r + TRANSPOSE_LEAD, 1)
             if r + 1 < PAIRS:
                 denominators(r + 1)
+            if 0 <= r - OM_LAG < PAIRS:
+                transpose_outputs(r - OM_LAG)
             if r < PAIRS:
-                normalise(r, 1, prod)
-            if 0 <= r - 1 < PAIRS:
-                transpose_outputs(r - 1)
+                normalise_vector(r, 0)
             if half_batch_due(r, QUANTISE_LAG) is not None:
                 quantise(half_batch_due(r, QUANTISE_LAG))
+            if r + 1 < PAIRS:
+                invert(r + 1)
+            if r < PAIRS:
+                normalise_vector(r, 1)
+            if half_batch_due(r, STORE_LAG) is not None:
+                store(half_batch_due(r, STORE_LAG))
+            if r < PAIRS:
+                normalise_scalar(r)
+            if r + TRANSPOSE_LEAD < PAIRS:
+                keep_queries(r + TRANSPOSE_LEAD)
+            if 0 <= r - OM_LAG < PAIRS:
+                regroup(r - OM_LAG)
 
         for pair in range(TRANSPOSE_LEAD):
             for cc in range(PAIR):
                 transpose_queries(pair, cc)
+            keep_queries(pair)
         denominators(0)
+        invert(0)
         for r in range(2):
             run_round(r)
 
-        wp_ps = psum.tile([P, WORD_BLOCKS, P], F32, tag="bank")
         wp_split = consts.tile([P, E], BF16)
         nc.vector.tensor_copy(
             out=wp_split[:].rearrange("p (u f) -> p u f", u=WORD_BLOCKS),
             in_=wp_rows[:].rearrange("p (f u) -> p u f", u=WORD_BLOCKS),
         )
+        wp_ps = psum.tile([P, WORD_BLOCKS, P], F32, tag="bank")
         wp_words = wp_split[:].bitcast(F32)
         for u in range(WORD_BLOCKS):
             nc.tensor.transpose(wp_ps[:, u, :], wp_words[:, u * P : (u + 1) * P], ident_f32[:])

@@ -199,11 +199,25 @@ def tile_linearattention_pb_t_kernel(tc, q, k_sum, context, Wp, bp, out):
                 nc.vector.scalar_tensor_tensor(out=om_out, in0=product, scalar=d_inv, in1=q_in, op0=MULT, op1=ADD)
 
         def normalise_scalar(pair):
-            for h in range(vector_heads(pair, 1), H):
-                om_out, product, d_inv, q_in = om_parts(pair, 1, h)
-                scaled = scaled_pool.tile([P, WORD_BLOCKS, D // WORD_BLOCKS], F32)
-                nc.scalar.activation(out=scaled[:], in_=product, func=COPY, scale=d_inv)
-                nc.gpsimd.tensor_tensor(out=om_out, in0=scaled[:], in1=q_in, op=ADD)
+            first = vector_heads(pair, 1)
+            half_head = D // WORD_BLOCKS
+            scaled = scaled_pool.tile([P, WORD_BLOCKS, H * half_head], F32)
+            for h in range(first, H):
+                product, d_inv = om_parts(pair, 1, h)[1:3]
+                nc.scalar.activation(
+                    out=scaled[:, :, h * half_head : (h + 1) * half_head], in_=product, func=COPY, scale=d_inv
+                )
+            heads = slice(first * half_head, H * half_head)
+            nc.gpsimd.tensor_tensor(
+                out=om_tiles[pair][:, 1, :]
+                .rearrange("p (u f) -> p u f", u=WORD_BLOCKS)[:, :, heads]
+                .rearrange("p u (h f) -> p u h f", f=half_head),
+                in0=scaled[:, :, heads].rearrange("p u (h f) -> p u h f", f=half_head),
+                in1=q_tiles[pair // PAIRS_PER_HALF][:, first:H, chunk_in_half(pair, 1), :].rearrange(
+                    "p h (f u) -> p u h f", u=WORD_BLOCKS
+                ),
+                op=ADD,
+            )
 
         def transpose_outputs(pair):
             om_words = om_tiles[pair][:].bitcast(F32)

@@ -28,20 +28,20 @@ PAIRS = B * PAIRS_PER_BATCH
 BIAS_ROW = B * H
 PSUM_BANKS = 8
 
-VECTOR_HEADS = (1, 2)
+SHARED_HEADS = (0, 1)
 
-TRANSPOSE_LEAD = 2
-OM_LAG = 2
-QUANTISE_LAG = OM_LAG + 2
-PROJECT_LAG = OM_LAG + 3
-STORE_LAG = OM_LAG + 4
+TRANSPOSE_LEAD = 3
+OM_LAG = 1
+QUANTISE_LAG = 4
+PROJECT_LAG = 6
 
-QT_BUFS = 4
-DINV_BUFS = 4
-SCALED_BUFS = 4
+QT_BUFS = 5
+DINV_BUFS = 3
 OM_BUFS = 5
 GROUPED_BUFS = 3
 MX_BUFS = 3
+RES_BUFS = 3
+SCALED_BUFS = 3
 OUT_BUFS = 16
 
 FLOPS = 2 * B * H * T * D * D + 2 * B * T * E * DIM
@@ -61,10 +61,11 @@ def tile_linearattention_pb_t_kernel(tc, q, k_sum, context, Wp, bp, out):
         q_pool = stack.enter_context(tc.tile_pool(name="q", bufs=HALVES))
         qT_pool = stack.enter_context(tc.tile_pool(name="qT", bufs=QT_BUFS))
         dinv_pool = stack.enter_context(tc.tile_pool(name="dinv", bufs=DINV_BUFS))
-        scaled_pool = stack.enter_context(tc.tile_pool(name="scaled", bufs=SCALED_BUFS))
         om_pool = stack.enter_context(tc.tile_pool(name="om", bufs=OM_BUFS))
         grouped_pool = stack.enter_context(tc.tile_pool(name="grouped", bufs=GROUPED_BUFS))
         mx_pool = stack.enter_context(tc.tile_pool(name="mx", bufs=MX_BUFS))
+        scaled_pool = stack.enter_context(tc.tile_pool(name="scaled", bufs=SCALED_BUFS))
+        res_pool = stack.enter_context(tc.tile_pool(name="res", bufs=RES_BUFS))
         out_pool = stack.enter_context(tc.tile_pool(name="out", bufs=OUT_BUFS))
         psum = stack.enter_context(tc.psum_pool(name="psum", bufs=PSUM_BANKS))
         stack.enter_context(tc.manual_schedule())
@@ -120,15 +121,13 @@ def tile_linearattention_pb_t_kernel(tc, q, k_sum, context, Wp, bp, out):
         grouped_tiles = {}
         mx_tiles = {}
         res_tiles = {}
+        res_sb_tiles = {}
 
         def chunk_in_half(pair, cc):
             return PAIR * (pair % PAIRS_PER_HALF) + cc
 
         def split_words(ap):
             return ap.rearrange("p (f u) -> p u f", u=WORD_BLOCKS)
-
-        def vector_heads(pair, cc):
-            return H if cc == 0 else VECTOR_HEADS[pair % 2]
 
         def transpose_queries(pair, cc):
             if cc == 0:
@@ -146,78 +145,79 @@ def tile_linearattention_pb_t_kernel(tc, q, k_sum, context, Wp, bp, out):
             nc.scalar.copy(out=qT[:], in_=tq_tiles[pair][:])
             qT_tiles[pair] = qT
 
-        def denominators(pair):
-            b = pair // PAIRS_PER_BATCH
-            den = psum.tile([P, PAIR, H], F32, tag="bank")
-            for cc in range(PAIR):
-                for h in range(H):
-                    nc.tensor.matmul(
-                        out=den[:, cc, h : h + 1],
-                        lhsT=qT_tiles[pair][:, cc, h, :],
-                        rhs=ksumT[:, b * H + h : b * H + h + 1],
-                        start=True,
-                        stop=True,
-                    )
-            den_tiles[pair] = den
+        def denominators(half_batch):
+            heads = half_batch // 2 * H
+            den = psum.tile([P, PAIRS_PER_HALF, PAIR, H], F32, tag="bank")
+            for i in range(PAIRS_PER_HALF):
+                for cc in range(PAIR):
+                    for h in range(H):
+                        nc.tensor.matmul(
+                            out=den[:, i, cc, h : h + 1],
+                            lhsT=qT_tiles[half_batch * PAIRS_PER_HALF + i][:, cc, h, :],
+                            rhs=ksumT[:, heads + h : heads + h + 1],
+                            start=True,
+                            stop=True,
+                        )
+            den_tiles[half_batch] = den
 
-        def invert(pair):
-            d_inv = dinv_pool.tile([P, PAIR, H], F32)
-            nc.vector.reciprocal(out=d_inv[:], in_=den_tiles[pair][:])
-            dinv_tiles[pair] = d_inv
+        def invert(half_batch):
+            d_inv = dinv_pool.tile([P, PAIRS_PER_HALF, PAIR, H], F32)
+            nc.vector.reciprocal(out=d_inv[:], in_=den_tiles[half_batch][:])
+            dinv_tiles[half_batch] = d_inv
 
-        def multiply(pair, cc):
-            b = pair // PAIRS_PER_BATCH
-            for heads in (range(vector_heads(pair, cc)), range(vector_heads(pair, cc), H)):
-                if len(heads) == 0:
-                    continue
-                product = psum.tile([P, H, D], F32, tag="bank")
-                for h in heads:
-                    nc.tensor.matmul(
-                        out=product[:, h, :],
-                        lhsT=qT_tiles[pair][:, cc, h, :],
-                        rhs=ctx[:, b * H + h, :],
-                        start=True,
-                        stop=True,
-                    )
-                    product_tiles[pair, cc, h] = product
+        def is_shared(pair, cc, h):
+            return cc == 1 and h >= H - SHARED_HEADS[pair % 2]
 
-        def om_parts(pair, cc, h):
+        def multiply(pair, cc, heads):
+            for h in heads:
+                if h > 0 and is_shared(pair, cc, h) == is_shared(pair, cc, h - 1):
+                    product_tiles[pair, cc, h] = product_tiles[pair, cc, h - 1]
+                else:
+                    product_new = psum.tile([P, H, D], F32, tag="bank")
+                    product_tiles[pair, cc, h] = product_new
+                nc.tensor.matmul(
+                    out=product_tiles[pair, cc, h][:, h, :],
+                    lhsT=qT_tiles[pair][:, cc, h, :],
+                    rhs=ctx[:, pair // PAIRS_PER_BATCH * H + h, :],
+                    start=True,
+                    stop=True,
+                )
+
+        def normalise(pair, cc, heads):
             if pair not in om_tiles:
                 om_new = om_pool.tile([P, PAIR, E], BF16)
                 om_tiles[pair] = om_new
             om_split = om_tiles[pair][:, cc, :].rearrange("p (u f) -> p u f", u=WORD_BLOCKS)
-            return (
-                om_split[:, :, h * D // WORD_BLOCKS : (h + 1) * D // WORD_BLOCKS],
-                split_words(product_tiles[pair, cc, h][:, h, :]),
-                dinv_tiles[pair][:, cc, h : h + 1],
-                split_words(q_tiles[pair // PAIRS_PER_HALF][:, h, chunk_in_half(pair, cc), :]),
-            )
-
-        def normalise_vector(pair, cc):
-            for h in range(vector_heads(pair, cc)):
-                om_out, product, d_inv, q_in = om_parts(pair, cc, h)
-                nc.vector.scalar_tensor_tensor(out=om_out, in0=product, scalar=d_inv, in1=q_in, op0=MULT, op1=ADD)
-
-        def normalise_scalar(pair):
-            first = vector_heads(pair, 1)
-            half_head = D // WORD_BLOCKS
-            scaled = scaled_pool.tile([P, WORD_BLOCKS, H * half_head], F32)
-            for h in range(first, H):
-                product, d_inv = om_parts(pair, 1, h)[1:3]
-                nc.scalar.activation(
-                    out=scaled[:, :, h * half_head : (h + 1) * half_head], in_=product, func=COPY, scale=d_inv
+            half_batch, i = divmod(pair, PAIRS_PER_HALF)
+            for h in heads:
+                if is_shared(pair, cc, h):
+                    continue
+                nc.vector.scalar_tensor_tensor(
+                    out=om_split[:, :, h * D // WORD_BLOCKS : (h + 1) * D // WORD_BLOCKS],
+                    in0=split_words(product_tiles[pair, cc, h][:, h, :]),
+                    scalar=dinv_tiles[half_batch][:, i, cc, h : h + 1],
+                    in1=split_words(q_tiles[half_batch][:, h, chunk_in_half(pair, cc), :]),
+                    op0=MULT,
+                    op1=ADD,
                 )
-            heads = slice(first * half_head, H * half_head)
-            nc.gpsimd.tensor_tensor(
-                out=om_tiles[pair][:, 1, :]
-                .rearrange("p (u f) -> p u f", u=WORD_BLOCKS)[:, :, heads]
-                .rearrange("p u (h f) -> p u h f", f=half_head),
-                in0=scaled[:, :, heads].rearrange("p u (h f) -> p u h f", f=half_head),
-                in1=q_tiles[pair // PAIRS_PER_HALF][:, first:H, chunk_in_half(pair, 1), :].rearrange(
-                    "p h (f u) -> p u h f", u=WORD_BLOCKS
-                ),
-                op=ADD,
-            )
+
+        def normalise_shared(pair):
+            half_batch, i = divmod(pair, PAIRS_PER_HALF)
+            om_split = om_tiles[pair][:, 1, :].rearrange("p (u f) -> p u f", u=WORD_BLOCKS)
+            for h in range(H - SHARED_HEADS[pair % 2], H):
+                scaled = scaled_pool.tile([P, D], F32)
+                nc.scalar.activation(
+                    out=scaled[:],
+                    in_=product_tiles[pair, 1, h][:, h, :],
+                    func=COPY,
+                    scale=dinv_tiles[half_batch][:, i, 1, h : h + 1],
+                )
+                nc.gpsimd.tensor_tensor(
+                    out=om_split[:, :, h * D // WORD_BLOCKS : (h + 1) * D // WORD_BLOCKS],
+                    in0=split_words(scaled[:]),
+                    in1=split_words(q_tiles[half_batch][:, h, chunk_in_half(pair, 1), :]),
+                    op=ADD,
+                )
 
         def transpose_outputs(pair):
             om_words = om_tiles[pair][:].bitcast(F32)
@@ -263,51 +263,62 @@ def tile_linearattention_pb_t_kernel(tc, q, k_sum, context, Wp, bp, out):
                 )
             res_tiles[half_batch] = res
 
+        def copy_result(half_batch):
+            res_sb = res_pool.tile([P, HALF, DIM], F32)
+            nc.scalar.copy(out=res_sb[:], in_=res_tiles[half_batch][:])
+            res_sb_tiles[half_batch] = res_sb
+
         def store(half_batch):
             out_sb = out_pool.tile([P, HALF, DIM], F32)
-            nc.vector.tensor_tensor(out=out_sb[:], in0=res_tiles[half_batch][:], in1=bias[:], op=ADD)
+            nc.gpsimd.tensor_tensor(out=out_sb[:], in0=res_sb_tiles[half_batch][:], in1=bias[:], op=ADD)
             b, half = divmod(half_batch, 2)
             out_by_token = out[b].rearrange("(p c) n -> p c n", c=CHUNKS)
             nc.sync.dma_start(out=out_by_token[:, half * HALF : (half + 1) * HALF, :], in_=out_sb[:])
 
         def run_round(r):
+            project_due = half_batch_due(r, PROJECT_LAG)
+            invert_due = half_batch_due(r + 1, 0)
             if r < PAIRS:
-                multiply(r, 0)
+                multiply(r, 0, range(0, H))
             if r + TRANSPOSE_LEAD < PAIRS:
                 transpose_queries(r + TRANSPOSE_LEAD, 0)
-            if half_batch_due(r, PROJECT_LAG) is not None:
-                project(half_batch_due(r, PROJECT_LAG))
+            if project_due is not None:
+                project(project_due)
             if r < PAIRS:
-                multiply(r, 1)
+                multiply(r, 1, range(0, H))
             if r + TRANSPOSE_LEAD < PAIRS:
                 transpose_queries(r + TRANSPOSE_LEAD, 1)
-            if r + 1 < PAIRS:
-                denominators(r + 1)
+            if invert_due is not None:
+                denominators(invert_due)
             if 0 <= r - OM_LAG < PAIRS:
                 transpose_outputs(r - OM_LAG)
-            if r < PAIRS:
-                normalise_vector(r, 0)
             if half_batch_due(r, QUANTISE_LAG) is not None:
                 quantise(half_batch_due(r, QUANTISE_LAG))
-            if r + 1 < PAIRS:
-                invert(r + 1)
             if r < PAIRS:
-                normalise_vector(r, 1)
-            if half_batch_due(r, STORE_LAG) is not None:
-                store(half_batch_due(r, STORE_LAG))
+                normalise(r, 0, range(0, H))
+                normalise(r, 1, range(0, H))
+            if invert_due is not None:
+                invert(invert_due)
             if r < PAIRS:
-                normalise_scalar(r)
+                normalise_shared(r)
+            if project_due is not None:
+                copy_result(project_due)
+                store(project_due)
             if r + TRANSPOSE_LEAD < PAIRS:
                 keep_queries(r + TRANSPOSE_LEAD)
             if 0 <= r - OM_LAG < PAIRS:
                 regroup(r - OM_LAG)
 
-        for pair in range(TRANSPOSE_LEAD):
+        for pair in range(PAIRS_PER_HALF):
             for cc in range(PAIR):
                 transpose_queries(pair, cc)
             keep_queries(pair)
         denominators(0)
         invert(0)
+        for pair in range(PAIRS_PER_HALF, TRANSPOSE_LEAD):
+            for cc in range(PAIR):
+                transpose_queries(pair, cc)
+            keep_queries(pair)
         for r in range(2):
             run_round(r)
 
@@ -329,5 +340,5 @@ def tile_linearattention_pb_t_kernel(tc, q, k_sum, context, Wp, bp, out):
         wp_scales = consts.tile([P, DIM], U8, align_bytes=64)
         nc.vector.quantize_mx(out=wp_codes[:].bitcast(FP8X4), scales=wp_scales[:], in_=wp_grouped[:])
 
-        for r in range(2, PAIRS - PAIRS_PER_HALF + STORE_LAG + 1):
+        for r in range(2, PAIRS - PAIRS_PER_HALF + PROJECT_LAG + 1):
             run_round(r)

@@ -82,11 +82,15 @@ def tile_linearattention_pb_t_kernel(tc, q, k_sum, context, Wp, bp, out):
             q_by_token = q[b].rearrange("h (p c) d -> p h c d", c=CHUNKS)
             for half in range(2):
                 q_half = q_pool.tile([P, H, HALF, D], BF16)
-                nc.sync.dma_start(out=q_half[:], in_=q_by_token[:, :, half * HALF : (half + 1) * HALF, :])
                 q_tiles.append(q_half)
-                if half == 0:
-                    heads = slice(b * H, (b + 1) * H)
-                    nc.sync.dma_start(out=ctx[:, heads, :], in_=context_by_feature[:, heads, :])
+                load = PAIR if len(q_tiles) == 1 else HALF
+                for c in range(0, HALF, load):
+                    nc.sync.dma_start(
+                        out=q_half[:, :, c : c + load, :], in_=q_by_token[:, :, half * HALF + c : half * HALF + c + load, :]
+                    )
+                    if half == 0 and c == 0:
+                        heads = slice(b * H, (b + 1) * H)
+                        nc.sync.dma_start(out=ctx[:, heads, :], in_=context_by_feature[:, heads, :])
             if b == 0:
                 nc.sync.dma_start(out=wp_rows[:], in_=Wp)
 
@@ -121,7 +125,6 @@ def tile_linearattention_pb_t_kernel(tc, q, k_sum, context, Wp, bp, out):
         grouped_tiles = {}
         mx_tiles = {}
         res_tiles = {}
-        res_sb_tiles = {}
 
         def chunk_in_half(pair, cc):
             return PAIR * (pair % PAIRS_PER_HALF) + cc
@@ -129,80 +132,82 @@ def tile_linearattention_pb_t_kernel(tc, q, k_sum, context, Wp, bp, out):
         def split_words(ap):
             return ap.rearrange("p (f u) -> p u f", u=WORD_BLOCKS)
 
-        def transpose_queries(pair, cc):
-            if cc == 0:
+        def transpose_query(pair, cc, h):
+            if (cc, h) == (0, 0):
                 tq_new = psum.tile([P, PAIR, H, P], BF16, tag="bank")
                 tq_tiles[pair] = tq_new
-            for h in range(H):
-                nc.tensor.transpose(
-                    tq_tiles[pair][:, cc, h, :],
-                    q_tiles[pair // PAIRS_PER_HALF][:, h, chunk_in_half(pair, cc), :],
-                    ident_bf16[:],
-                )
+            nc.tensor.transpose(
+                tq_tiles[pair][:, cc, h, :],
+                q_tiles[pair // PAIRS_PER_HALF][:, h, chunk_in_half(pair, cc), :],
+                ident_bf16[:],
+            )
 
-        def keep_queries(pair):
-            qT = qT_pool.tile([P, PAIR, H, P], BF16)
-            nc.scalar.copy(out=qT[:], in_=tq_tiles[pair][:])
-            qT_tiles[pair] = qT
+        def keep_queries(pair, chunks):
+            if chunks.start == 0:
+                qT_new = qT_pool.tile([P, PAIR, H, P], BF16)
+                qT_tiles[pair] = qT_new
+            part = slice(chunks.start, chunks.stop)
+            nc.scalar.copy(out=qT_tiles[pair][:, part, :, :], in_=tq_tiles[pair][:, part, :, :])
 
-        def denominators(half_batch):
-            heads = half_batch // 2 * H
+        def denominators(half_batch, pairs):
             den = psum.tile([P, PAIRS_PER_HALF, PAIR, H], F32, tag="bank")
-            for i in range(PAIRS_PER_HALF):
+            for i in pairs:
                 for cc in range(PAIR):
                     for h in range(H):
+                        head = half_batch // 2 * H + h
                         nc.tensor.matmul(
                             out=den[:, i, cc, h : h + 1],
                             lhsT=qT_tiles[half_batch * PAIRS_PER_HALF + i][:, cc, h, :],
-                            rhs=ksumT[:, heads + h : heads + h + 1],
+                            rhs=ksumT[:, head : head + 1],
                             start=True,
                             stop=True,
                         )
             den_tiles[half_batch] = den
 
-        def invert(half_batch):
+        def invert(half_batch, pairs):
+            part = slice(pairs.start, pairs.stop)
             d_inv = dinv_pool.tile([P, PAIRS_PER_HALF, PAIR, H], F32)
-            nc.vector.reciprocal(out=d_inv[:], in_=den_tiles[half_batch][:])
-            dinv_tiles[half_batch] = d_inv
+            nc.vector.reciprocal(out=d_inv[:, part, :, :], in_=den_tiles[half_batch][:, part, :, :])
+            for i in pairs:
+                dinv_tiles[half_batch * PAIRS_PER_HALF + i] = d_inv[:, i, :, :]
 
         def is_shared(pair, cc, h):
             return cc == 1 and h >= H - SHARED_HEADS[pair % 2]
 
-        def multiply(pair, cc, heads):
-            for h in heads:
-                if h > 0 and is_shared(pair, cc, h) == is_shared(pair, cc, h - 1):
-                    product_tiles[pair, cc, h] = product_tiles[pair, cc, h - 1]
-                else:
-                    product_new = psum.tile([P, H, D], F32, tag="bank")
-                    product_tiles[pair, cc, h] = product_new
-                nc.tensor.matmul(
-                    out=product_tiles[pair, cc, h][:, h, :],
-                    lhsT=qT_tiles[pair][:, cc, h, :],
-                    rhs=ctx[:, pair // PAIRS_PER_BATCH * H + h, :],
-                    start=True,
-                    stop=True,
-                )
+        def multiply(pair, cc, h):
+            if h > 0 and is_shared(pair, cc, h) == is_shared(pair, cc, h - 1):
+                product_tiles[pair, cc, h] = product_tiles[pair, cc, h - 1]
+            else:
+                product_new = psum.tile([P, H, D], F32, tag="bank")
+                product_tiles[pair, cc, h] = product_new
+            nc.tensor.matmul(
+                out=product_tiles[pair, cc, h][:, h, :],
+                lhsT=qT_tiles[pair][:, cc, h, :],
+                rhs=ctx[:, pair // PAIRS_PER_BATCH * H + h, :],
+                start=True,
+                stop=True,
+            )
 
-        def normalise(pair, cc, heads):
+        def normalise(pair, cc):
             if pair not in om_tiles:
                 om_new = om_pool.tile([P, PAIR, E], BF16)
                 om_tiles[pair] = om_new
             om_split = om_tiles[pair][:, cc, :].rearrange("p (u f) -> p u f", u=WORD_BLOCKS)
-            half_batch, i = divmod(pair, PAIRS_PER_HALF)
-            for h in heads:
+            half_batch = pair // PAIRS_PER_HALF
+            for h in range(H):
                 if is_shared(pair, cc, h):
                     continue
                 nc.vector.scalar_tensor_tensor(
                     out=om_split[:, :, h * D // WORD_BLOCKS : (h + 1) * D // WORD_BLOCKS],
                     in0=split_words(product_tiles[pair, cc, h][:, h, :]),
-                    scalar=dinv_tiles[half_batch][:, i, cc, h : h + 1],
+                    scalar=dinv_tiles[pair][:, cc, h : h + 1],
                     in1=split_words(q_tiles[half_batch][:, h, chunk_in_half(pair, cc), :]),
                     op0=MULT,
                     op1=ADD,
                 )
 
         def normalise_shared(pair):
-            half_batch, i = divmod(pair, PAIRS_PER_HALF)
+            half_batch = pair // PAIRS_PER_HALF
             om_split = om_tiles[pair][:, 1, :].rearrange("p (u f) -> p u f", u=WORD_BLOCKS)
             for h in range(H - SHARED_HEADS[pair % 2], H):
                 scaled = scaled_pool.tile([P, D], F32)
@@ -210,7 +215,7 @@ def tile_linearattention_pb_t_kernel(tc, q, k_sum, context, Wp, bp, out):
                     out=scaled[:],
                     in_=product_tiles[pair, 1, h][:, h, :],
                     func=COPY,
-                    scale=dinv_tiles[half_batch][:, i, 1, h : h + 1],
+                    scale=dinv_tiles[pair][:, 1, h : h + 1],
                 )
                 nc.gpsimd.tensor_tensor(
                     out=om_split[:, :, h * D // WORD_BLOCKS : (h + 1) * D // WORD_BLOCKS],
@@ -241,19 +246,23 @@ def tile_linearattention_pb_t_kernel(tc, q, k_sum, context, Wp, bp, out):
                 out=grouped_words[:, first : first + PAIR, :, :], in_=tom_tiles[pair][:].rearrange("p c u t -> p c t u")
             )
 
-        def quantise(half_batch):
-            codes = mx_pool.tile([P, HALF * P], U32, align_bytes=64)
-            scales = mx_pool.tile([P, HALF * P], U8, align_bytes=64)
-            nc.vector.quantize_mx(out=codes[:].bitcast(FP8X4), scales=scales[:], in_=grouped_tiles[half_batch][:])
-            mx_tiles[half_batch] = (codes, scales)
+        def quantise(half_batch, chunks):
+            codes = mx_pool.tile([P, len(chunks) * P], U32, align_bytes=64, name="codes%d" % len(chunks))
+            scales = mx_pool.tile([P, len(chunks) * P], U8, align_bytes=64, name="scales%d" % len(chunks))
+            nc.vector.quantize_mx(
+                out=codes[:].bitcast(FP8X4),
+                scales=scales[:],
+                in_=grouped_tiles[half_batch][:, chunks.start * P * PACK : chunks.stop * P * PACK],
+            )
+            mx_tiles[half_batch, chunks.start] = (codes, scales)
 
-        def project(half_batch):
-            codes, scales = mx_tiles[half_batch]
+        def project(half_batch, chunks):
+            codes, scales = mx_tiles[half_batch, chunks.start]
             res = psum.tile([P, HALF, DIM], F32, tag="bank")
-            for c in range(HALF):
-                tokens = slice(c * P, (c + 1) * P)
+            for i in range(len(chunks)):
+                tokens = slice(i * P, (i + 1) * P)
                 nc.tensor.matmul_mx(
-                    out=res[:, c, :],
+                    out=res[:, i, :],
                     lhsT=codes[:, tokens].bitcast(FP8X4),
                     lhsT_scale=scales[:, tokens],
                     rhs=wp_codes[:].bitcast(FP8X4),
@@ -261,64 +270,82 @@ def tile_linearattention_pb_t_kernel(tc, q, k_sum, context, Wp, bp, out):
                     start=True,
                     stop=True,
                 )
-            res_tiles[half_batch] = res
+            res_tiles[half_batch, chunks.start] = res
 
-        def copy_result(half_batch):
-            res_sb = res_pool.tile([P, HALF, DIM], F32)
-            nc.scalar.copy(out=res_sb[:], in_=res_tiles[half_batch][:])
-            res_sb_tiles[half_batch] = res_sb
-
-        def store(half_batch):
-            out_sb = out_pool.tile([P, HALF, DIM], F32)
-            nc.gpsimd.tensor_tensor(out=out_sb[:], in0=res_sb_tiles[half_batch][:], in1=bias[:], op=ADD)
+        def store(half_batch, chunks, out_sb):
             b, half = divmod(half_batch, 2)
+            first = half * HALF + chunks.start
             out_by_token = out[b].rearrange("(p c) n -> p c n", c=CHUNKS)
-            nc.sync.dma_start(out=out_by_token[:, half * HALF : (half + 1) * HALF, :], in_=out_sb[:])
+            nc.sync.dma_start(out=out_by_token[:, first : first + len(chunks), :], in_=out_sb[:, 0 : len(chunks), :])
+
+        def finish_on_gpsimd(half_batch):
+            res_sb = res_pool.tile([P, HALF, DIM], F32)
+            nc.scalar.copy(out=res_sb[:], in_=res_tiles[half_batch, 0][:])
+            out_sb = out_pool.tile([P, HALF, DIM], F32)
+            nc.gpsimd.tensor_tensor(out=out_sb[:], in0=res_sb[:], in1=bias[:], op=ADD)
+            store(half_batch, range(HALF), out_sb)
+
+        def finish_on_vector(half_batch, chunks):
+            n = len(chunks)
+            out_sb = out_pool.tile([P, HALF, DIM], F32)
+            nc.vector.tensor_tensor(
+                out=out_sb[:, 0:n, :], in0=res_tiles[half_batch, chunks.start][:, 0:n, :], in1=bias[:, 0:n, :], op=ADD
+            )
+            store(half_batch, chunks, out_sb)
+
+        def queries_due(r):
+            first = PAIRS_PER_HALF if r == 0 else r + TRANSPOSE_LEAD
+            pairs = range(first, min(r + TRANSPOSE_LEAD + 1, PAIRS))
+            return [(pair, cc, h) for pair in pairs for cc in range(PAIR) for h in range(H)]
 
         def run_round(r):
             project_due = half_batch_due(r, PROJECT_LAG)
             invert_due = half_batch_due(r + 1, 0)
-            if r < PAIRS:
-                multiply(r, 0, range(0, H))
-            if r + TRANSPOSE_LEAD < PAIRS:
-                transpose_queries(r + TRANSPOSE_LEAD, 0)
-            if project_due is not None:
-                project(project_due)
-            if r < PAIRS:
-                multiply(r, 1, range(0, H))
-            if r + TRANSPOSE_LEAD < PAIRS:
-                transpose_queries(r + TRANSPOSE_LEAD, 1)
+            invert_pairs = range(PAIRS_PER_HALF)
+            if r == 0:
+                invert_due = 0
+                invert_pairs = range(1, PAIRS_PER_HALF)
+            queries = queries_due(r)
+            woven = 0
+            for cc in range(PAIR):
+                for h in range(H):
+                    multiply(r, cc, h)
+                    if (cc, h) == (0, H - 1):
+                        if project_due is not None:
+                            project(project_due, range(HALF))
+                    elif woven < len(queries):
+                        transpose_query(*queries[woven])
+                        woven += 1
+            for query in queries[woven:]:
+                transpose_query(*query)
             if invert_due is not None:
-                denominators(invert_due)
-            if 0 <= r - OM_LAG < PAIRS:
+                denominators(invert_due, invert_pairs)
+            if r >= OM_LAG:
                 transpose_outputs(r - OM_LAG)
             if half_batch_due(r, QUANTISE_LAG) is not None:
-                quantise(half_batch_due(r, QUANTISE_LAG))
-            if r < PAIRS:
-                normalise(r, 0, range(0, H))
-                normalise(r, 1, range(0, H))
+                quantise(half_batch_due(r, QUANTISE_LAG), range(HALF))
+            for cc in range(PAIR):
+                normalise(r, cc)
             if invert_due is not None:
-                invert(invert_due)
-            if r < PAIRS:
-                normalise_shared(r)
+                invert(invert_due, invert_pairs)
+            normalise_shared(r)
             if project_due is not None:
-                copy_result(project_due)
-                store(project_due)
-            if r + TRANSPOSE_LEAD < PAIRS:
-                keep_queries(r + TRANSPOSE_LEAD)
-            if 0 <= r - OM_LAG < PAIRS:
+                finish_on_gpsimd(project_due)
+            for pair in sorted(set([query[0] for query in queries_due(r)])):
+                keep_queries(pair, range(PAIR))
+            if r >= OM_LAG:
                 regroup(r - OM_LAG)
 
         for pair in range(PAIRS_PER_HALF):
             for cc in range(PAIR):
-                transpose_queries(pair, cc)
-            keep_queries(pair)
-        denominators(0)
-        invert(0)
-        for pair in range(PAIRS_PER_HALF, TRANSPOSE_LEAD):
-            for cc in range(PAIR):
-                transpose_queries(pair, cc)
-            keep_queries(pair)
+                for h in range(H):
+                    transpose_query(pair, cc, h)
+                if pair == 0:
+                    keep_queries(pair, range(cc, cc + 1))
+            if pair > 0:
+                keep_queries(pair, range(PAIR))
+        denominators(0, range(0, 1))
+        invert(0, range(0, 1))
         for r in range(2):
             run_round(r)
 
@@ -340,5 +367,21 @@ def tile_linearattention_pb_t_kernel(tc, q, k_sum, context, Wp, bp, out):
         wp_scales = consts.tile([P, DIM], U8, align_bytes=64)
         nc.vector.quantize_mx(out=wp_codes[:].bitcast(FP8X4), scales=wp_scales[:], in_=wp_grouped[:])
 
-        for r in range(2, PAIRS - PAIRS_PER_HALF + PROJECT_LAG + 1):
+        for r in range(2, PAIRS):
             run_round(r)
+
+        last = HALVES - 1
+        transpose_outputs(PAIRS - 1)
+        regroup(PAIRS - 1)
+        quantise(last - 1, range(HALF))
+        parts = [range(c, c + PAIR) for c in range(0, HALF, PAIR)]
+        for part in parts:
+            quantise(last, part)
+        project(last - 2, range(HALF))
+        finish_on_gpsimd(last - 2)
+        project(last - 1, range(HALF))
+        for part in parts:
+            project(last, part)
+        finish_on_vector(last - 1, range(HALF))
+        for part in parts:
+            finish_on_vector(last, part)

@@ -44,6 +44,8 @@ RES_BUFS = 3
 SCALED_BUFS = 3
 OUT_BUFS = 16
 
+WP_ROUND = 3
+
 FLOPS = 2 * B * H * T * D * D + 2 * B * T * E * DIM
 
 
@@ -72,8 +74,6 @@ def tile_linearattention_pb_t_kernel(tc, q, k_sum, context, Wp, bp, out):
 
         small_rows = consts.tile([P, D], BF16)
         nc.vector.memset(small_rows[:], 0.0)
-        nc.sync.dma_start(out=small_rows[0:BIAS_ROW, :], in_=k_sum.rearrange("b h o d -> (b h o) d"))
-        nc.sync.dma_start(out=small_rows[BIAS_ROW : BIAS_ROW + 1, :], in_=bp.rearrange("(o n) -> o n", o=1))
         wp_rows = consts.tile([P, E], BF16)
         ctx = consts.tile([P, B * H, D], BF16)
         q_tiles = []
@@ -83,37 +83,27 @@ def tile_linearattention_pb_t_kernel(tc, q, k_sum, context, Wp, bp, out):
             for half in range(2):
                 q_half = q_pool.tile([P, H, HALF, D], BF16)
                 q_tiles.append(q_half)
-                load = PAIR if len(q_tiles) == 1 else HALF
+                load = PAIR if b < 2 else HALF
                 for c in range(0, HALF, load):
-                    nc.sync.dma_start(
-                        out=q_half[:, :, c : c + load, :], in_=q_by_token[:, :, half * HALF + c : half * HALF + c + load, :]
-                    )
-                    if half == 0 and c == 0:
+                    first = half * HALF + c
+                    nc.sync.dma_start(out=q_half[:, :, c : c + load, :], in_=q_by_token[:, :, first : first + load, :])
+                    if first == 0:
+                        if b == 0:
+                            nc.sync.dma_start(
+                                out=small_rows[0:BIAS_ROW, :], in_=k_sum.rearrange("b h o d -> (b h o) d")
+                            )
+                            nc.sync.dma_start(
+                                out=small_rows[BIAS_ROW : BIAS_ROW + 1, :], in_=bp.rearrange("(o n) -> o n", o=1)
+                            )
                         heads = slice(b * H, (b + 1) * H)
                         nc.sync.dma_start(out=ctx[:, heads, :], in_=context_by_feature[:, heads, :])
-            if b == 0:
-                nc.sync.dma_start(out=wp_rows[:], in_=Wp)
+                if b == 1 and half == 0:
+                    nc.sync.dma_start(out=wp_rows[:], in_=Wp)
 
         ident_bf16 = consts.tile([P, P], BF16)
         make_identity(nc, ident_bf16[:])
         ident_f32 = consts.tile([P, P], F32)
         make_identity(nc, ident_f32[:])
-
-        small_ps = psum.tile([P, P], BF16, tag="bank")
-        nc.tensor.transpose(small_ps[:], small_rows[:], ident_bf16[:])
-        ksumT = consts.tile([P, B * H], BF16)
-        nc.vector.tensor_copy(out=ksumT[:], in_=small_ps[:, 0:BIAS_ROW])
-        bias_ps = psum.tile([P, DIM], F32, tag="bank")
-        nc.tensor.matmul(
-            out=bias_ps[:],
-            lhsT=ident_bf16[:, BIAS_ROW : BIAS_ROW + 1].to_broadcast([P, P]),
-            rhs=small_rows[:],
-            start=True,
-            stop=True,
-        )
-        bias = consts.tile([P, HALF, DIM], F32)
-        for c in range(HALF):
-            nc.vector.tensor_copy(out=bias[:, c, :], in_=bias_ps[:])
 
         tq_tiles = {}
         qT_tiles = {}
@@ -224,16 +214,16 @@ def tile_linearattention_pb_t_kernel(tc, q, k_sum, context, Wp, bp, out):
                     op=ADD,
                 )
 
-        def transpose_outputs(pair):
+        def transpose_outputs(pair, chunks=range(PAIR)):
             om_words = om_tiles[pair][:].bitcast(F32)
             tom = psum.tile([P, PAIR, WORD_BLOCKS, P], F32, tag="bank")
-            for cc in range(PAIR):
+            for cc in chunks:
                 for u in range(WORD_BLOCKS):
                     nc.tensor.transpose(tom[:, cc, u, :], om_words[:, cc, u * P : (u + 1) * P], ident_f32[:])
-            tom_tiles[pair] = tom
+            tom_tiles[pair, chunks.start] = tom
 
-        def regroup(pair):
-            if pair % PAIRS_PER_HALF == 0:
+        def regroup(pair, chunks=range(PAIR)):
+            if pair % PAIRS_PER_HALF == 0 and chunks.start == 0:
                 grouped_new = grouped_pool.tile([P, HALF * P * PACK], BF16, align_bytes=64)
                 grouped_tiles[pair // PAIRS_PER_HALF] = grouped_new
             grouped_words = (
@@ -241,9 +231,10 @@ def tile_linearattention_pb_t_kernel(tc, q, k_sum, context, Wp, bp, out):
                 .bitcast(F32)
                 .rearrange("p (c t u) -> p c t u", c=HALF, u=WORD_BLOCKS)
             )
-            first = chunk_in_half(pair, 0)
+            first = chunk_in_half(pair, chunks.start)
             nc.scalar.copy(
-                out=grouped_words[:, first : first + PAIR, :, :], in_=tom_tiles[pair][:].rearrange("p c u t -> p c t u")
+                out=grouped_words[:, first : first + len(chunks), :, :],
+                in_=tom_tiles[pair, chunks.start][:, chunks.start : chunks.stop, :, :].rearrange("p c u t -> p c t u"),
             )
 
         def quantise(half_batch, chunks):
@@ -282,24 +273,25 @@ def tile_linearattention_pb_t_kernel(tc, q, k_sum, context, Wp, bp, out):
             res_sb = res_pool.tile([P, HALF, DIM], F32)
             nc.scalar.copy(out=res_sb[:], in_=res_tiles[half_batch, 0][:])
             out_sb = out_pool.tile([P, HALF, DIM], F32)
-            nc.gpsimd.tensor_tensor(out=out_sb[:], in0=res_sb[:], in1=bias[:], op=ADD)
+            nc.gpsimd.tensor_tensor(out=out_sb[:], in0=res_sb[:], in1=bias_for(HALF), op=ADD)
             store(half_batch, range(HALF), out_sb)
 
         def finish_on_vector(half_batch, chunks):
             n = len(chunks)
             out_sb = out_pool.tile([P, HALF, DIM], F32)
             nc.vector.tensor_tensor(
-                out=out_sb[:, 0:n, :], in0=res_tiles[half_batch, chunks.start][:, 0:n, :], in1=bias[:, 0:n, :], op=ADD
+                out=out_sb[:, 0:n, :], in0=res_tiles[half_batch, chunks.start][:, 0:n, :], in1=bias_for(n), op=ADD
             )
             store(half_batch, chunks, out_sb)
 
         def queries_due(r):
-            first = PAIRS_PER_HALF if r == 0 else r + TRANSPOSE_LEAD
-            pairs = range(first, min(r + TRANSPOSE_LEAD + 1, PAIRS))
+            pairs = range(1 if r == 0 else r + TRANSPOSE_LEAD, min(r + TRANSPOSE_LEAD + 1, PAIRS))
             return [(pair, cc, h) for pair in pairs for cc in range(PAIR) for h in range(H)]
 
         def run_round(r):
-            project_due = half_batch_due(r, PROJECT_LAG)
+            stage_round = PAIRS if r == PAIRS - 1 else r
+            quantise_due = half_batch_due(stage_round, QUANTISE_LAG)
+            project_due = half_batch_due(stage_round, PROJECT_LAG)
             invert_due = half_batch_due(r + 1, 0)
             invert_pairs = range(PAIRS_PER_HALF)
             if r == 0:
@@ -318,12 +310,15 @@ def tile_linearattention_pb_t_kernel(tc, q, k_sum, context, Wp, bp, out):
                         woven += 1
             for query in queries[woven:]:
                 transpose_query(*query)
+            if r == 0:
+                for pair in sorted(set([query[0] for query in queries_due(r)])):
+                    keep_queries(pair, range(PAIR))
             if invert_due is not None:
                 denominators(invert_due, invert_pairs)
             if r >= OM_LAG:
                 transpose_outputs(r - OM_LAG)
-            if half_batch_due(r, QUANTISE_LAG) is not None:
-                quantise(half_batch_due(r, QUANTISE_LAG), range(HALF))
+            if quantise_due is not None:
+                quantise(quantise_due, range(HALF))
             for cc in range(PAIR):
                 normalise(r, cc)
             if invert_due is not None:
@@ -331,57 +326,83 @@ def tile_linearattention_pb_t_kernel(tc, q, k_sum, context, Wp, bp, out):
             normalise_shared(r)
             if project_due is not None:
                 finish_on_gpsimd(project_due)
-            for pair in sorted(set([query[0] for query in queries_due(r)])):
-                keep_queries(pair, range(PAIR))
+            if r > 0:
+                for pair in sorted(set([query[0] for query in queries_due(r)])):
+                    keep_queries(pair, range(PAIR))
             if r >= OM_LAG:
                 regroup(r - OM_LAG)
 
-        for pair in range(PAIRS_PER_HALF):
-            for cc in range(PAIR):
-                for h in range(H):
-                    transpose_query(pair, cc, h)
-                if pair == 0:
-                    keep_queries(pair, range(cc, cc + 1))
-            if pair > 0:
-                keep_queries(pair, range(PAIR))
-        denominators(0, range(0, 1))
-        invert(0, range(0, 1))
-        for r in range(2):
-            run_round(r)
-
         wp_split = consts.tile([P, E], BF16)
-        nc.vector.tensor_copy(
-            out=wp_split[:].rearrange("p (u f) -> p u f", u=WORD_BLOCKS),
-            in_=wp_rows[:].rearrange("p (f u) -> p u f", u=WORD_BLOCKS),
-        )
-        wp_ps = psum.tile([P, WORD_BLOCKS, P], F32, tag="bank")
-        wp_words = wp_split[:].bitcast(F32)
-        for u in range(WORD_BLOCKS):
-            nc.tensor.transpose(wp_ps[:, u, :], wp_words[:, u * P : (u + 1) * P], ident_f32[:])
         wp_grouped = consts.tile([P, DIM * PACK], BF16, align_bytes=64)
-        nc.vector.tensor_copy(
-            out=wp_grouped[:].bitcast(F32).rearrange("p (n u) -> p n u", u=WORD_BLOCKS),
-            in_=wp_ps[:].rearrange("p u n -> p n u"),
-        )
         wp_codes = consts.tile([P, DIM], U32, align_bytes=64)
         wp_scales = consts.tile([P, DIM], U8, align_bytes=64)
-        nc.vector.quantize_mx(out=wp_codes[:].bitcast(FP8X4), scales=wp_scales[:], in_=wp_grouped[:])
 
-        for r in range(2, PAIRS):
+        def split_weights():
+            nc.gpsimd.tensor_copy(
+                out=wp_split[:].rearrange("p (u f) -> p u f", u=WORD_BLOCKS),
+                in_=wp_rows[:].rearrange("p (f u) -> p u f", u=WORD_BLOCKS),
+            )
+
+        def turn_weights():
+            wp_ps = psum.tile([P, WORD_BLOCKS, P], F32, tag="bank")
+            wp_words = wp_split[:].bitcast(F32)
+            for u in range(WORD_BLOCKS):
+                nc.tensor.transpose(wp_ps[:, u, :], wp_words[:, u * P : (u + 1) * P], ident_f32[:])
+            nc.scalar.copy(
+                out=wp_grouped[:].bitcast(F32).rearrange("p (n u) -> p n u", u=WORD_BLOCKS),
+                in_=wp_ps[:].rearrange("p u n -> p n u"),
+            )
+
+        bias = consts.tile([P, DIM], F32)
+
+        def spread_bias():
+            bias_ps = psum.tile([P, DIM], F32, tag="bank")
+            nc.tensor.matmul(
+                out=bias_ps[:],
+                lhsT=ident_bf16[:, BIAS_ROW : BIAS_ROW + 1].to_broadcast([P, P]),
+                rhs=small_rows[:],
+                start=True,
+                stop=True,
+            )
+            nc.scalar.copy(out=bias[:], in_=bias_ps[:])
+
+        def bias_for(n):
+            return bias[:].unsqueeze(1).to_broadcast([P, n, DIM])
+
+        def quantise_weights():
+            nc.vector.quantize_mx(out=wp_codes[:].bitcast(FP8X4), scales=wp_scales[:], in_=wp_grouped[:])
+
+        for cc in range(PAIR):
+            for h in range(H):
+                transpose_query(0, cc, h)
+            keep_queries(0, range(cc, cc + 1))
+        small_ps = psum.tile([P, P], BF16, tag="bank")
+        nc.tensor.transpose(small_ps[:], small_rows[:], ident_bf16[:])
+        ksumT = consts.tile([P, B * H], BF16)
+        nc.vector.tensor_copy(out=ksumT[:], in_=small_ps[:, 0:BIAS_ROW])
+        denominators(0, range(0, 1))
+        invert(0, range(0, 1))
+        for r in range(PAIRS):
             run_round(r)
+            if r == WP_ROUND - 2:
+                split_weights()
+            if r == WP_ROUND - 1:
+                spread_bias()
+            if r == WP_ROUND:
+                turn_weights()
+            if r == WP_ROUND + 1:
+                quantise_weights()
 
         last = HALVES - 1
-        transpose_outputs(PAIRS - 1)
-        regroup(PAIRS - 1)
-        quantise(last - 1, range(HALF))
-        parts = [range(c, c + PAIR) for c in range(0, HALF, PAIR)]
+        project(last - 1, range(HALF))
+        for cc in range(PAIR):
+            transpose_outputs(PAIRS - 1, range(cc, cc + 1))
+            regroup(PAIRS - 1, range(cc, cc + 1))
+        parts = [range(0, 2), range(2, 3), range(3, 4)]
         for part in parts:
             quantise(last, part)
-        project(last - 2, range(HALF))
-        finish_on_gpsimd(last - 2)
-        project(last - 1, range(HALF))
-        for part in parts:
             project(last, part)
-        finish_on_vector(last - 1, range(HALF))
+            if part.start == 0:
+                finish_on_vector(last - 1, range(HALF))
         for part in parts:
             finish_on_vector(last, part)

@@ -27,24 +27,26 @@ HALVES = 2 * B
 PAIRS = B * PAIRS_PER_BATCH
 BIAS_ROW = B * H
 PSUM_BANKS = 8
-
-SHARED_HEADS = (0, 1)
+BANK = 512
+WIDE_HEADS = H - 1
+WIDE = BANK // WIDE_HEADS
+CTX_ROW = D + 8
 
 TRANSPOSE_LEAD = 3
 OM_LAG = 1
 QUANTISE_LAG = 4
 PROJECT_LAG = 6
+SPLIT_ROUND, TURN_ROUND, WEIGHTS_ROUND = 1, 3, 4
 
 QT_BUFS = 5
 DINV_BUFS = 3
-OM_BUFS = 5
+WIDE_DINV_BUFS = 3
+OM_BUFS = 4
 GROUPED_BUFS = 3
 MX_BUFS = 3
-RES_BUFS = 3
 SCALED_BUFS = 3
+RES_BUFS = 3
 OUT_BUFS = 16
-
-WP_ROUND = 3
 
 FLOPS = 2 * B * H * T * D * D + 2 * B * T * E * DIM
 
@@ -56,6 +58,14 @@ def half_batch_due(r, lag):
     return None
 
 
+def is_shared(pair, cc, h):
+    return (pair % 2, cc, h) == (1, PAIR - 1, H - 1)
+
+
+def is_wide(pair, cc, h):
+    return pair % 2 == 1 and cc == PAIR - 1 and h < WIDE_HEADS
+
+
 def tile_linearattention_pb_t_kernel(tc, q, k_sum, context, Wp, bp, out):
     nc = tc.nc
     with ExitStack() as stack:
@@ -63,6 +73,7 @@ def tile_linearattention_pb_t_kernel(tc, q, k_sum, context, Wp, bp, out):
         q_pool = stack.enter_context(tc.tile_pool(name="q", bufs=HALVES))
         qT_pool = stack.enter_context(tc.tile_pool(name="qT", bufs=QT_BUFS))
         dinv_pool = stack.enter_context(tc.tile_pool(name="dinv", bufs=DINV_BUFS))
+        wide_dinv_pool = stack.enter_context(tc.tile_pool(name="wide_dinv", bufs=WIDE_DINV_BUFS))
         om_pool = stack.enter_context(tc.tile_pool(name="om", bufs=OM_BUFS))
         grouped_pool = stack.enter_context(tc.tile_pool(name="grouped", bufs=GROUPED_BUFS))
         mx_pool = stack.enter_context(tc.tile_pool(name="mx", bufs=MX_BUFS))
@@ -75,9 +86,9 @@ def tile_linearattention_pb_t_kernel(tc, q, k_sum, context, Wp, bp, out):
         small_rows = consts.tile([P, D], BF16)
         nc.vector.memset(small_rows[:], 0.0)
         wp_rows = consts.tile([P, E], BF16)
-        ctx = consts.tile([P, B * H, D], BF16)
-        q_tiles = []
+        ctx = consts.tile([P, B * H, CTX_ROW], BF16)
         context_by_feature = context.rearrange("b h d e -> d (b h) e")
+        q_tiles = []
         for b in range(B):
             q_by_token = q[b].rearrange("h (p c) d -> p h c d", c=CHUNKS)
             for half in range(2):
@@ -87,29 +98,71 @@ def tile_linearattention_pb_t_kernel(tc, q, k_sum, context, Wp, bp, out):
                 for c in range(0, HALF, load):
                     first = half * HALF + c
                     nc.sync.dma_start(out=q_half[:, :, c : c + load, :], in_=q_by_token[:, :, first : first + load, :])
+                    if (b, first) == (0, 0):
+                        nc.sync.dma_start(out=small_rows[0:BIAS_ROW, :], in_=k_sum.rearrange("b h o d -> (b h o) d"))
+                        nc.sync.dma_start(
+                            out=small_rows[BIAS_ROW : BIAS_ROW + 1, :], in_=bp.rearrange("(o n) -> o n", o=1)
+                        )
                     if first == 0:
-                        if b == 0:
-                            nc.sync.dma_start(
-                                out=small_rows[0:BIAS_ROW, :], in_=k_sum.rearrange("b h o d -> (b h o) d")
-                            )
-                            nc.sync.dma_start(
-                                out=small_rows[BIAS_ROW : BIAS_ROW + 1, :], in_=bp.rearrange("(o n) -> o n", o=1)
-                            )
                         heads = slice(b * H, (b + 1) * H)
-                        nc.sync.dma_start(out=ctx[:, heads, :], in_=context_by_feature[:, heads, :])
-                if b == 1 and half == 0:
+                        nc.sync.dma_start(out=ctx[:, heads, 0:D], in_=context_by_feature[:, heads, :])
+                if (b, half) == (1, 0):
                     nc.sync.dma_start(out=wp_rows[:], in_=Wp)
 
         ident_bf16 = consts.tile([P, P], BF16)
         make_identity(nc, ident_bf16[:])
         ident_f32 = consts.tile([P, P], F32)
         make_identity(nc, ident_f32[:])
+        wp_split = consts.tile([P, E], BF16)
+        wp_grouped = consts.tile([P, DIM * PACK], BF16, align_bytes=64)
+        wp_codes = consts.tile([P, DIM], U32, align_bytes=64)
+        wp_scales = consts.tile([P, DIM], U8, align_bytes=64)
+        bias = consts.tile([P, DIM], F32)
+
+        def turn_k_sum():
+            small_ps = psum.tile([P, P], BF16, tag="bank")
+            nc.tensor.transpose(small_ps[:], small_rows[:], ident_bf16[:])
+            nc.vector.tensor_copy(out=ctx[:, :, D], in_=small_ps[:, 0:BIAS_ROW])
+
+        def spread_bias():
+            bias_ps = psum.tile([P, DIM], F32, tag="bank")
+            nc.tensor.matmul(
+                out=bias_ps[:],
+                lhsT=ident_bf16[:, BIAS_ROW : BIAS_ROW + 1].to_broadcast([P, P]),
+                rhs=small_rows[:],
+                start=True,
+                stop=True,
+            )
+            nc.scalar.copy(out=bias[:], in_=bias_ps[:])
+
+        def bias_for(n):
+            return bias[:].unsqueeze(1).to_broadcast([P, n, DIM])
+
+        def split_weights():
+            nc.gpsimd.tensor_copy(
+                out=wp_split[:].rearrange("p (u f) -> p u f", u=WORD_BLOCKS),
+                in_=wp_rows[:].rearrange("p (f u) -> p u f", u=WORD_BLOCKS),
+            )
+
+        def turn_weights():
+            wp_ps = psum.tile([P, WORD_BLOCKS, P], F32, tag="bank")
+            wp_words = wp_split[:].bitcast(F32)
+            for u in range(WORD_BLOCKS):
+                nc.tensor.transpose(wp_ps[:, u, :], wp_words[:, u * P : (u + 1) * P], ident_f32[:])
+            nc.scalar.copy(
+                out=wp_grouped[:].bitcast(F32).rearrange("p (n u) -> p n u", u=WORD_BLOCKS),
+                in_=wp_ps[:].rearrange("p u n -> p n u"),
+            )
+
+        def quantise_weights():
+            nc.vector.quantize_mx(out=wp_codes[:].bitcast(FP8X4), scales=wp_scales[:], in_=wp_grouped[:])
 
         tq_tiles = {}
         qT_tiles = {}
         den_tiles = {}
-        dinv_tiles = {}
-        product_tiles = {}
+        d_inv_of = {}
+        bank_of = {}
+        product_of = {}
         om_tiles = {}
         tom_tiles = {}
         grouped_tiles = {}
@@ -121,6 +174,9 @@ def tile_linearattention_pb_t_kernel(tc, q, k_sum, context, Wp, bp, out):
 
         def split_words(ap):
             return ap.rearrange("p (f u) -> p u f", u=WORD_BLOCKS)
+
+        def context_row(pair, h):
+            return pair // PAIRS_PER_BATCH * H + h
 
         def transpose_query(pair, cc, h):
             if (cc, h) == (0, 0):
@@ -139,82 +195,85 @@ def tile_linearattention_pb_t_kernel(tc, q, k_sum, context, Wp, bp, out):
             part = slice(chunks.start, chunks.stop)
             nc.scalar.copy(out=qT_tiles[pair][:, part, :, :], in_=tq_tiles[pair][:, part, :, :])
 
-        def denominators(half_batch, pairs):
-            den = psum.tile([P, PAIRS_PER_HALF, PAIR, H], F32, tag="bank")
-            for i in pairs:
-                for cc in range(PAIR):
-                    for h in range(H):
-                        head = half_batch // 2 * H + h
-                        nc.tensor.matmul(
-                            out=den[:, i, cc, h : h + 1],
-                            lhsT=qT_tiles[half_batch * PAIRS_PER_HALF + i][:, cc, h, :],
-                            rhs=ksumT[:, head : head + 1],
-                            start=True,
-                            stop=True,
-                        )
-            den_tiles[half_batch] = den
+        def lone_denominators(pairs):
+            return [
+                (pair, cc, h) for pair in pairs for cc in range(PAIR) for h in range(H) if not is_wide(pair, cc, h)
+            ]
 
-        def invert(half_batch, pairs):
-            part = slice(pairs.start, pairs.stop)
-            d_inv = dinv_pool.tile([P, PAIRS_PER_HALF, PAIR, H], F32)
-            nc.vector.reciprocal(out=d_inv[:, part, :, :], in_=den_tiles[half_batch][:, part, :, :])
-            for i in pairs:
-                dinv_tiles[half_batch * PAIRS_PER_HALF + i] = d_inv[:, i, :, :]
+        def denominators(pairs):
+            den = psum.tile([P, HALF * H], F32, tag="bank")
+            for column, (pair, cc, h) in enumerate(lone_denominators(pairs)):
+                nc.tensor.matmul(
+                    out=den[:, column : column + 1],
+                    lhsT=qT_tiles[pair][:, cc, h, :],
+                    rhs=ctx[:, context_row(pair, h), D : D + 1],
+                    start=True,
+                    stop=True,
+                )
+            den_tiles[pairs.start] = den
 
-        def is_shared(pair, cc, h):
-            return cc == 1 and h >= H - SHARED_HEADS[pair % 2]
+        def invert(pairs):
+            heads = lone_denominators(pairs)
+            n = len(heads)
+            d_inv = dinv_pool.tile([P, HALF * H], F32)
+            nc.vector.reciprocal(out=d_inv[:, 0:n], in_=den_tiles[pairs.start][:, 0:n])
+            for column, head in enumerate(heads):
+                d_inv_of[head] = d_inv[:, column : column + 1]
+
+        def invert_wide(pair):
+            d_inv = wide_dinv_pool.tile([P, WIDE_HEADS], F32)
+            nc.vector.reciprocal(out=d_inv[:], in_=bank_of[pair, PAIR - 1, 0][:, :, D])
+            for h in range(WIDE_HEADS):
+                d_inv_of[pair, PAIR - 1, h] = d_inv[:, h : h + 1]
 
         def multiply(pair, cc, h):
-            if h > 0 and is_shared(pair, cc, h) == is_shared(pair, cc, h - 1):
-                product_tiles[pair, cc, h] = product_tiles[pair, cc, h - 1]
+            wide = is_wide(pair, cc, h)
+            if h > 0 and not is_shared(pair, cc, h):
+                bank_of[pair, cc, h] = bank_of[pair, cc, h - 1]
+            elif wide:
+                wide_new = psum.tile([P, WIDE_HEADS, WIDE], F32, tag="bank")
+                bank_of[pair, cc, h] = wide_new
             else:
-                product_new = psum.tile([P, H, D], F32, tag="bank")
-                product_tiles[pair, cc, h] = product_new
+                bank_new = psum.tile([P, H, D], F32, tag="bank")
+                bank_of[pair, cc, h] = bank_new
+            columns = D + 1 if wide else D
             nc.tensor.matmul(
-                out=product_tiles[pair, cc, h][:, h, :],
+                out=bank_of[pair, cc, h][:, h, 0:columns],
                 lhsT=qT_tiles[pair][:, cc, h, :],
-                rhs=ctx[:, pair // PAIRS_PER_BATCH * H + h, :],
+                rhs=ctx[:, context_row(pair, h), 0:columns],
                 start=True,
                 stop=True,
             )
+            product_of[pair, cc, h] = bank_of[pair, cc, h][:, h, 0:D]
 
-        def normalise(pair, cc):
+        def om_parts(pair, cc, h):
             if pair not in om_tiles:
                 om_new = om_pool.tile([P, PAIR, E], BF16)
                 om_tiles[pair] = om_new
             om_split = om_tiles[pair][:, cc, :].rearrange("p (u f) -> p u f", u=WORD_BLOCKS)
-            half_batch = pair // PAIRS_PER_HALF
-            for h in range(H):
-                if is_shared(pair, cc, h):
-                    continue
-                nc.vector.scalar_tensor_tensor(
-                    out=om_split[:, :, h * D // WORD_BLOCKS : (h + 1) * D // WORD_BLOCKS],
-                    in0=split_words(product_tiles[pair, cc, h][:, h, :]),
-                    scalar=dinv_tiles[pair][:, cc, h : h + 1],
-                    in1=split_words(q_tiles[half_batch][:, h, chunk_in_half(pair, cc), :]),
-                    op0=MULT,
-                    op1=ADD,
-                )
+            return (
+                om_split[:, :, h * D // WORD_BLOCKS : (h + 1) * D // WORD_BLOCKS],
+                split_words(q_tiles[pair // PAIRS_PER_HALF][:, h, chunk_in_half(pair, cc), :]),
+            )
 
-        def normalise_shared(pair):
-            half_batch = pair // PAIRS_PER_HALF
-            om_split = om_tiles[pair][:, 1, :].rearrange("p (u f) -> p u f", u=WORD_BLOCKS)
-            for h in range(H - SHARED_HEADS[pair % 2], H):
-                scaled = scaled_pool.tile([P, D], F32)
-                nc.scalar.activation(
-                    out=scaled[:],
-                    in_=product_tiles[pair, 1, h][:, h, :],
-                    func=COPY,
-                    scale=dinv_tiles[pair][:, 1, h : h + 1],
-                )
-                nc.gpsimd.tensor_tensor(
-                    out=om_split[:, :, h * D // WORD_BLOCKS : (h + 1) * D // WORD_BLOCKS],
-                    in0=split_words(scaled[:]),
-                    in1=split_words(q_tiles[half_batch][:, h, chunk_in_half(pair, 1), :]),
-                    op=ADD,
-                )
+        def normalise(pair, cc, h):
+            om_out, q_in = om_parts(pair, cc, h)
+            nc.vector.scalar_tensor_tensor(
+                out=om_out,
+                in0=split_words(product_of[pair, cc, h]),
+                scalar=d_inv_of[pair, cc, h],
+                in1=q_in,
+                op0=MULT,
+                op1=ADD,
+            )
 
-        def transpose_outputs(pair, chunks=range(PAIR)):
+        def normalise_shared(pair, cc, h):
+            om_out, q_in = om_parts(pair, cc, h)
+            scaled = scaled_pool.tile([P, D], F32)
+            nc.scalar.activation(out=scaled[:], in_=product_of[pair, cc, h], func=COPY, scale=d_inv_of[pair, cc, h])
+            nc.gpsimd.tensor_tensor(out=om_out, in0=split_words(scaled[:]), in1=q_in, op=ADD)
+
+        def transpose_outputs(pair, chunks):
             om_words = om_tiles[pair][:].bitcast(F32)
             tom = psum.tile([P, PAIR, WORD_BLOCKS, P], F32, tag="bank")
             for cc in chunks:
@@ -222,14 +281,13 @@ def tile_linearattention_pb_t_kernel(tc, q, k_sum, context, Wp, bp, out):
                     nc.tensor.transpose(tom[:, cc, u, :], om_words[:, cc, u * P : (u + 1) * P], ident_f32[:])
             tom_tiles[pair, chunks.start] = tom
 
-        def regroup(pair, chunks=range(PAIR)):
-            if pair % PAIRS_PER_HALF == 0 and chunks.start == 0:
+        def regroup(pair, chunks):
+            half_batch = pair // PAIRS_PER_HALF
+            if half_batch not in grouped_tiles:
                 grouped_new = grouped_pool.tile([P, HALF * P * PACK], BF16, align_bytes=64)
-                grouped_tiles[pair // PAIRS_PER_HALF] = grouped_new
+                grouped_tiles[half_batch] = grouped_new
             grouped_words = (
-                grouped_tiles[pair // PAIRS_PER_HALF][:]
-                .bitcast(F32)
-                .rearrange("p (c t u) -> p c t u", c=HALF, u=WORD_BLOCKS)
+                grouped_tiles[half_batch][:].bitcast(F32).rearrange("p (c t u) -> p c t u", c=HALF, u=WORD_BLOCKS)
             )
             first = chunk_in_half(pair, chunks.start)
             nc.scalar.copy(
@@ -238,8 +296,9 @@ def tile_linearattention_pb_t_kernel(tc, q, k_sum, context, Wp, bp, out):
             )
 
         def quantise(half_batch, chunks):
-            codes = mx_pool.tile([P, len(chunks) * P], U32, align_bytes=64, name="codes%d" % len(chunks))
-            scales = mx_pool.tile([P, len(chunks) * P], U8, align_bytes=64, name="scales%d" % len(chunks))
+            columns = len(chunks) * P
+            codes = mx_pool.tile([P, columns], U32, align_bytes=64, name="codes%d" % len(chunks))
+            scales = mx_pool.tile([P, columns], U8, align_bytes=64, name="scales%d" % len(chunks))
             nc.vector.quantize_mx(
                 out=codes[:].bitcast(FP8X4),
                 scales=scales[:],
@@ -285,19 +344,21 @@ def tile_linearattention_pb_t_kernel(tc, q, k_sum, context, Wp, bp, out):
             store(half_batch, chunks, out_sb)
 
         def queries_due(r):
-            pairs = range(1 if r == 0 else r + TRANSPOSE_LEAD, min(r + TRANSPOSE_LEAD + 1, PAIRS))
-            return [(pair, cc, h) for pair in pairs for cc in range(PAIR) for h in range(H)]
+            return range(1 if r == 0 else r + TRANSPOSE_LEAD, min(r + TRANSPOSE_LEAD + 1, PAIRS))
+
+        def inverses_due(r):
+            if r == 0:
+                return range(1, PAIRS_PER_HALF)
+            if (r + 1) % PAIRS_PER_HALF == 0 and r + 1 < PAIRS:
+                return range(r + 1, r + 1 + PAIRS_PER_HALF)
+            return range(0)
 
         def run_round(r):
             stage_round = PAIRS if r == PAIRS - 1 else r
             quantise_due = half_batch_due(stage_round, QUANTISE_LAG)
             project_due = half_batch_due(stage_round, PROJECT_LAG)
-            invert_due = half_batch_due(r + 1, 0)
-            invert_pairs = range(PAIRS_PER_HALF)
-            if r == 0:
-                invert_due = 0
-                invert_pairs = range(1, PAIRS_PER_HALF)
-            queries = queries_due(r)
+
+            queries = [(pair, cc, h) for pair in queries_due(r) for cc in range(PAIR) for h in range(H)]
             woven = 0
             for cc in range(PAIR):
                 for h in range(H):
@@ -311,86 +372,51 @@ def tile_linearattention_pb_t_kernel(tc, q, k_sum, context, Wp, bp, out):
             for query in queries[woven:]:
                 transpose_query(*query)
             if r == 0:
-                for pair in sorted(set([query[0] for query in queries_due(r)])):
+                for pair in queries_due(r):
                     keep_queries(pair, range(PAIR))
-            if invert_due is not None:
-                denominators(invert_due, invert_pairs)
+            if len(inverses_due(r)) > 0:
+                denominators(inverses_due(r))
             if r >= OM_LAG:
-                transpose_outputs(r - OM_LAG)
+                transpose_outputs(r - OM_LAG, range(PAIR))
+
             if quantise_due is not None:
                 quantise(quantise_due, range(HALF))
             for cc in range(PAIR):
-                normalise(r, cc)
-            if invert_due is not None:
-                invert(invert_due, invert_pairs)
-            normalise_shared(r)
+                for h in range(H):
+                    if (cc, h) == (0, H - 1) and is_wide(r, PAIR - 1, 0):
+                        invert_wide(r)
+                    if not is_shared(r, cc, h):
+                        normalise(r, cc, h)
+            if len(inverses_due(r)) > 0:
+                invert(inverses_due(r))
+
+            if is_shared(r, PAIR - 1, H - 1):
+                normalise_shared(r, PAIR - 1, H - 1)
             if project_due is not None:
                 finish_on_gpsimd(project_due)
             if r > 0:
-                for pair in sorted(set([query[0] for query in queries_due(r)])):
+                for pair in queries_due(r):
                     keep_queries(pair, range(PAIR))
             if r >= OM_LAG:
-                regroup(r - OM_LAG)
-
-        wp_split = consts.tile([P, E], BF16)
-        wp_grouped = consts.tile([P, DIM * PACK], BF16, align_bytes=64)
-        wp_codes = consts.tile([P, DIM], U32, align_bytes=64)
-        wp_scales = consts.tile([P, DIM], U8, align_bytes=64)
-
-        def split_weights():
-            nc.gpsimd.tensor_copy(
-                out=wp_split[:].rearrange("p (u f) -> p u f", u=WORD_BLOCKS),
-                in_=wp_rows[:].rearrange("p (f u) -> p u f", u=WORD_BLOCKS),
-            )
-
-        def turn_weights():
-            wp_ps = psum.tile([P, WORD_BLOCKS, P], F32, tag="bank")
-            wp_words = wp_split[:].bitcast(F32)
-            for u in range(WORD_BLOCKS):
-                nc.tensor.transpose(wp_ps[:, u, :], wp_words[:, u * P : (u + 1) * P], ident_f32[:])
-            nc.scalar.copy(
-                out=wp_grouped[:].bitcast(F32).rearrange("p (n u) -> p n u", u=WORD_BLOCKS),
-                in_=wp_ps[:].rearrange("p u n -> p n u"),
-            )
-
-        bias = consts.tile([P, DIM], F32)
-
-        def spread_bias():
-            bias_ps = psum.tile([P, DIM], F32, tag="bank")
-            nc.tensor.matmul(
-                out=bias_ps[:],
-                lhsT=ident_bf16[:, BIAS_ROW : BIAS_ROW + 1].to_broadcast([P, P]),
-                rhs=small_rows[:],
-                start=True,
-                stop=True,
-            )
-            nc.scalar.copy(out=bias[:], in_=bias_ps[:])
-
-        def bias_for(n):
-            return bias[:].unsqueeze(1).to_broadcast([P, n, DIM])
-
-        def quantise_weights():
-            nc.vector.quantize_mx(out=wp_codes[:].bitcast(FP8X4), scales=wp_scales[:], in_=wp_grouped[:])
+                regroup(r - OM_LAG, range(PAIR))
 
         for cc in range(PAIR):
             for h in range(H):
                 transpose_query(0, cc, h)
             keep_queries(0, range(cc, cc + 1))
-        small_ps = psum.tile([P, P], BF16, tag="bank")
-        nc.tensor.transpose(small_ps[:], small_rows[:], ident_bf16[:])
-        ksumT = consts.tile([P, B * H], BF16)
-        nc.vector.tensor_copy(out=ksumT[:], in_=small_ps[:, 0:BIAS_ROW])
-        denominators(0, range(0, 1))
-        invert(0, range(0, 1))
+        turn_k_sum()
+        denominators(range(0, 1))
+        invert(range(0, 1))
+
         for r in range(PAIRS):
             run_round(r)
-            if r == WP_ROUND - 2:
+            if r == SPLIT_ROUND:
                 split_weights()
-            if r == WP_ROUND - 1:
+            if r == TURN_ROUND - 1:
                 spread_bias()
-            if r == WP_ROUND:
+            if r == TURN_ROUND:
                 turn_weights()
-            if r == WP_ROUND + 1:
+            if r == WEIGHTS_ROUND:
                 quantise_weights()
 
         last = HALVES - 1
@@ -398,7 +424,7 @@ def tile_linearattention_pb_t_kernel(tc, q, k_sum, context, Wp, bp, out):
         for cc in range(PAIR):
             transpose_outputs(PAIRS - 1, range(cc, cc + 1))
             regroup(PAIRS - 1, range(cc, cc + 1))
-        parts = [range(0, 2), range(2, 3), range(3, 4)]
+        parts = [range(0, PAIR)] + [range(c, c + 1) for c in range(PAIR, HALF)]
         for part in parts:
             quantise(last, part)
             project(last, part)

@@ -383,7 +383,7 @@ def tile_linearattention_pb_t_kernel(tc, q, k_sum, context, Wp, bp, out):
                 quantise(quantise_due, range(HALF))
             for cc in range(PAIR):
                 for h in range(H):
-                    if (cc, h) == (0, H - 1) and is_wide(r, PAIR - 1, 0):
+                    if (cc, h) == (0, H - 2) and is_wide(r, PAIR - 1, 0):
                         invert_wide(r)
                     if not is_shared(r, cc, h):
                         normalise(r, cc, h)
@@ -392,7 +392,7 @@ def tile_linearattention_pb_t_kernel(tc, q, k_sum, context, Wp, bp, out):
 
             if is_shared(r, PAIR - 1, H - 1):
                 normalise_shared(r, PAIR - 1, H - 1)
-            if project_due is not None:
+            if project_due is not None and r < PAIRS - 1:
                 finish_on_gpsimd(project_due)
             if r > 0:
                 for pair in queries_due(r):
@@ -420,6 +420,7 @@ def tile_linearattention_pb_t_kernel(tc, q, k_sum, context, Wp, bp, out):
                 quantise_weights()
 
         last = HALVES - 1
+        finish_on_vector(last - 2, range(HALF))
         project(last - 1, range(HALF))
         for cc in range(PAIR):
             transpose_outputs(PAIRS - 1, range(cc, cc + 1))

from contextlib import ExitStack

import concourse.mybir as mybir
from concourse.masks import make_identity

BF16 = mybir.dt.bfloat16
F32 = mybir.dt.float32
U32 = mybir.dt.uint32
U8 = mybir.dt.uint8
FP8X4 = mybir.dt.float8_e4m3fn_x4
COPY = mybir.ActivationFunctionType.Copy
MULT = mybir.AluOpType.mult
ADD = mybir.AluOpType.add

B, H, T, D = 16, 4, 1024, 128
DIM = 128
E = H * D
P = 128
PACK = 4
WORD_BLOCKS = 2
CHUNKS = T // P
PAIR = 2
HALF = CHUNKS // 2
PAIRS_PER_BATCH = CHUNKS // PAIR
PAIRS_PER_HALF = HALF // PAIR
HALVES = 2 * B
PAIRS = B * PAIRS_PER_BATCH
BIAS_ROW = B * H
PSUM_BANKS = 8
BANK = 512
WIDE_HEADS = H - 1
WIDE = BANK // WIDE_HEADS
CTX_ROW = D + 8

TRANSPOSE_LEAD = 3
OM_LAG = 1
QUANTISE_LAG = 4
PROJECT_LAG = 6
SPLIT_ROUND, TURN_ROUND, WEIGHTS_ROUND = 1, 3, 4

QT_BUFS = 5
DINV_BUFS = 3
WIDE_DINV_BUFS = 3
OM_BUFS = 4
GROUPED_BUFS = 3
MX_BUFS = 3
SCALED_BUFS = 3
RES_BUFS = 3
OUT_BUFS = 16

FLOPS = 2 * B * H * T * D * D + 2 * B * T * E * DIM


def half_batch_due(r, lag):
    first_round = r - lag
    if first_round % PAIRS_PER_HALF == 0 and 0 <= first_round < PAIRS:
        return first_round // PAIRS_PER_HALF
    return None


def is_shared(pair, cc, h):
    return (pair % 2, cc, h) == (1, PAIR - 1, H - 1)


def is_wide(pair, cc, h):
    return pair % 2 == 1 and cc == PAIR - 1 and h < WIDE_HEADS


def tile_linearattention_pb_t_kernel(tc, q, k_sum, context, Wp, bp, out):
    nc = tc.nc
    with ExitStack() as stack:
        consts = stack.enter_context(tc.tile_pool(name="consts", bufs=1))
        q_pool = stack.enter_context(tc.tile_pool(name="q", bufs=HALVES))
        qT_pool = stack.enter_context(tc.tile_pool(name="qT", bufs=QT_BUFS))
        dinv_pool = stack.enter_context(tc.tile_pool(name="dinv", bufs=DINV_BUFS))
        wide_dinv_pool = stack.enter_context(tc.tile_pool(name="wide_dinv", bufs=WIDE_DINV_BUFS))
        om_pool = stack.enter_context(tc.tile_pool(name="om", bufs=OM_BUFS))
        grouped_pool = stack.enter_context(tc.tile_pool(name="grouped", bufs=GROUPED_BUFS))
        mx_pool = stack.enter_context(tc.tile_pool(name="mx", bufs=MX_BUFS))
        scaled_pool = stack.enter_context(tc.tile_pool(name="scaled", bufs=SCALED_BUFS))
        res_pool = stack.enter_context(tc.tile_pool(name="res", bufs=RES_BUFS))
        out_pool = stack.enter_context(tc.tile_pool(name="out", bufs=OUT_BUFS))
        psum = stack.enter_context(tc.psum_pool(name="psum", bufs=PSUM_BANKS))
        stack.enter_context(tc.manual_schedule())

        small_rows = consts.tile([P, D], BF16)
        nc.vector.memset(small_rows[:], 0.0)
        wp_rows = consts.tile([P, E], BF16)
        ctx = consts.tile([P, B * H, CTX_ROW], BF16)
        context_by_feature = context.rearrange("b h d e -> d (b h) e")
        q_tiles = []
        for b in range(B):
            q_by_token = q[b].rearrange("h (p c) d -> p h c d", c=CHUNKS)
            for half in range(2):
                q_half = q_pool.tile([P, H, HALF, D], BF16)
                q_tiles.append(q_half)
                load = PAIR if b < 2 else HALF
                for c in range(0, HALF, load):
                    first = half * HALF + c
                    nc.sync.dma_start(out=q_half[:, :, c : c + load, :], in_=q_by_token[:, :, first : first + load, :])
                    if (b, first) == (0, 0):
                        nc.sync.dma_start(out=small_rows[0:BIAS_ROW, :], in_=k_sum.rearrange("b h o d -> (b h o) d"))
                        nc.sync.dma_start(
                            out=small_rows[BIAS_ROW : BIAS_ROW + 1, :], in_=bp.rearrange("(o n) -> o n", o=1)
                        )
                    if first == 0:
                        heads = slice(b * H, (b + 1) * H)
                        nc.sync.dma_start(out=ctx[:, heads, 0:D], in_=context_by_feature[:, heads, :])
                if (b, half) == (1, 0):
                    nc.sync.dma_start(out=wp_rows[:], in_=Wp)

        ident_bf16 = consts.tile([P, P], BF16)
        make_identity(nc, ident_bf16[:])
        ident_f32 = consts.tile([P, P], F32)
        make_identity(nc, ident_f32[:])
        wp_split = consts.tile([P, E], BF16)
        wp_grouped = consts.tile([P, DIM * PACK], BF16, align_bytes=64)
        wp_codes = consts.tile([P, DIM], U32, align_bytes=64)
        wp_scales = consts.tile([P, DIM], U8, align_bytes=64)
        bias = consts.tile([P, DIM], F32)

        def turn_k_sum():
            small_ps = psum.tile([P, P], BF16, tag="bank")
            nc.tensor.transpose(small_ps[:], small_rows[:], ident_bf16[:])
            nc.vector.tensor_copy(out=ctx[:, :, D], in_=small_ps[:, 0:BIAS_ROW])

        def spread_bias():
            bias_ps = psum.tile([P, DIM], F32, tag="bank")
            nc.tensor.matmul(
                out=bias_ps[:],
                lhsT=ident_bf16[:, BIAS_ROW : BIAS_ROW + 1].to_broadcast([P, P]),
                rhs=small_rows[:],
                start=True,
                stop=True,
            )
            nc.scalar.copy(out=bias[:], in_=bias_ps[:])

        def bias_for(n):
            return bias[:].unsqueeze(1).to_broadcast([P, n, DIM])

        def split_weights():
            nc.gpsimd.tensor_copy(
                out=wp_split[:].rearrange("p (u f) -> p u f", u=WORD_BLOCKS),
                in_=wp_rows[:].rearrange("p (f u) -> p u f", u=WORD_BLOCKS),
            )

        def turn_weights():
            wp_ps = psum.tile([P, WORD_BLOCKS, P], F32, tag="bank")
            wp_words = wp_split[:].bitcast(F32)
            for u in range(WORD_BLOCKS):
                nc.tensor.transpose(wp_ps[:, u, :], wp_words[:, u * P : (u + 1) * P], ident_f32[:])
            nc.scalar.copy(
                out=wp_grouped[:].bitcast(F32).rearrange("p (n u) -> p n u", u=WORD_BLOCKS),
                in_=wp_ps[:].rearrange("p u n -> p n u"),
            )

        def quantise_weights():
            nc.vector.quantize_mx(out=wp_codes[:].bitcast(FP8X4), scales=wp_scales[:], in_=wp_grouped[:])

        tq_tiles = {}
        qT_tiles = {}
        den_tiles = {}
        d_inv_of = {}
        bank_of = {}
        product_of = {}
        om_tiles = {}
        tom_tiles = {}
        grouped_tiles = {}
        mx_tiles = {}
        res_tiles = {}

        def chunk_in_half(pair, cc):
            return PAIR * (pair % PAIRS_PER_HALF) + cc

        def split_words(ap):
            return ap.rearrange("p (f u) -> p u f", u=WORD_BLOCKS)

        def context_row(pair, h):
            return pair // PAIRS_PER_BATCH * H + h

        def transpose_query(pair, cc, h):
            if (cc, h) == (0, 0):
                tq_new = psum.tile([P, PAIR, H, P], BF16, tag="bank")
                tq_tiles[pair] = tq_new
            nc.tensor.transpose(
                tq_tiles[pair][:, cc, h, :],
                q_tiles[pair // PAIRS_PER_HALF][:, h, chunk_in_half(pair, cc), :],
                ident_bf16[:],
            )

        def keep_queries(pair, chunks):
            if chunks.start == 0:
                qT_new = qT_pool.tile([P, PAIR, H, P], BF16)
                qT_tiles[pair] = qT_new
            part = slice(chunks.start, chunks.stop)
            nc.scalar.copy(out=qT_tiles[pair][:, part, :, :], in_=tq_tiles[pair][:, part, :, :])

        def lone_denominators(pairs):
            return [
                (pair, cc, h) for pair in pairs for cc in range(PAIR) for h in range(H) if not is_wide(pair, cc, h)
            ]

        def denominators(pairs):
            den = psum.tile([P, HALF * H], F32, tag="bank")
            for column, (pair, cc, h) in enumerate(lone_denominators(pairs)):
                nc.tensor.matmul(
                    out=den[:, column : column + 1],
                    lhsT=qT_tiles[pair][:, cc, h, :],
                    rhs=ctx[:, context_row(pair, h), D : D + 1],
                    start=True,
                    stop=True,
                )
            den_tiles[pairs.start] = den

        def invert(pairs):
            heads = lone_denominators(pairs)
            n = len(heads)
            d_inv = dinv_pool.tile([P, HALF * H], F32)
            nc.vector.reciprocal(out=d_inv[:, 0:n], in_=den_tiles[pairs.start][:, 0:n])
            for column, head in enumerate(heads):
                d_inv_of[head] = d_inv[:, column : column + 1]

        def invert_wide(pair):
            d_inv = wide_dinv_pool.tile([P, WIDE_HEADS], F32)
            nc.vector.reciprocal(out=d_inv[:], in_=bank_of[pair, PAIR - 1, 0][:, :, D])
            for h in range(WIDE_HEADS):
                d_inv_of[pair, PAIR - 1, h] = d_inv[:, h : h + 1]

        def multiply(pair, cc, h):
            wide = is_wide(pair, cc, h)
            if h > 0 and not is_shared(pair, cc, h):
                bank_of[pair, cc, h] = bank_of[pair, cc, h - 1]
            elif wide:
                wide_new = psum.tile([P, WIDE_HEADS, WIDE], F32, tag="bank")
                bank_of[pair, cc, h] = wide_new
            else:
                bank_new = psum.tile([P, H, D], F32, tag="bank")
                bank_of[pair, cc, h] = bank_new
            columns = D + 1 if wide else D
            nc.tensor.matmul(
                out=bank_of[pair, cc, h][:, h, 0:columns],
                lhsT=qT_tiles[pair][:, cc, h, :],
                rhs=ctx[:, context_row(pair, h), 0:columns],
                start=True,
                stop=True,
            )
            product_of[pair, cc, h] = bank_of[pair, cc, h][:, h, 0:D]

        def om_parts(pair, cc, h):
            if pair not in om_tiles:
                om_new = om_pool.tile([P, PAIR, E], BF16)
                om_tiles[pair] = om_new
            om_split = om_tiles[pair][:, cc, :].rearrange("p (u f) -> p u f", u=WORD_BLOCKS)
            return (
                om_split[:, :, h * D // WORD_BLOCKS : (h + 1) * D // WORD_BLOCKS],
                split_words(q_tiles[pair // PAIRS_PER_HALF][:, h, chunk_in_half(pair, cc), :]),
            )

        def normalise(pair, cc, h):
            om_out, q_in = om_parts(pair, cc, h)
            nc.vector.scalar_tensor_tensor(
                out=om_out,
                in0=split_words(product_of[pair, cc, h]),
                scalar=d_inv_of[pair, cc, h],
                in1=q_in,
                op0=MULT,
                op1=ADD,
            )

        def normalise_shared(pair, cc, h):
            om_out, q_in = om_parts(pair, cc, h)
            scaled = scaled_pool.tile([P, D], F32)
            nc.scalar.activation(out=scaled[:], in_=product_of[pair, cc, h], func=COPY, scale=d_inv_of[pair, cc, h])
            nc.gpsimd.tensor_tensor(out=om_out, in0=split_words(scaled[:]), in1=q_in, op=ADD)

        def transpose_outputs(pair, chunks):
            om_words = om_tiles[pair][:].bitcast(F32)
            tom = psum.tile([P, PAIR, WORD_BLOCKS, P], F32, tag="bank")
            for cc in chunks:
                for u in range(WORD_BLOCKS):
                    nc.tensor.transpose(tom[:, cc, u, :], om_words[:, cc, u * P : (u + 1) * P], ident_f32[:])
            tom_tiles[pair, chunks.start] = tom

        def regroup(pair, chunks):
            half_batch = pair // PAIRS_PER_HALF
            if half_batch not in grouped_tiles:
                grouped_new = grouped_pool.tile([P, HALF * P * PACK], BF16, align_bytes=64)
                grouped_tiles[half_batch] = grouped_new
            grouped_words = (
                grouped_tiles[half_batch][:].bitcast(F32).rearrange("p (c t u) -> p c t u", c=HALF, u=WORD_BLOCKS)
            )
            first = chunk_in_half(pair, chunks.start)
            nc.scalar.copy(
                out=grouped_words[:, first : first + len(chunks), :, :],
                in_=tom_tiles[pair, chunks.start][:, chunks.start : chunks.stop, :, :].rearrange("p c u t -> p c t u"),
            )

        def quantise(half_batch, chunks):
            columns = len(chunks) * P
            codes = mx_pool.tile([P, columns], U32, align_bytes=64, name="codes%d" % len(chunks))
            scales = mx_pool.tile([P, columns], U8, align_bytes=64, name="scales%d" % len(chunks))
            nc.vector.quantize_mx(
                out=codes[:].bitcast(FP8X4),
                scales=scales[:],
                in_=grouped_tiles[half_batch][:, chunks.start * P * PACK : chunks.stop * P * PACK],
            )
            mx_tiles[half_batch, chunks.start] = (codes, scales)

        def project(half_batch, chunks):
            codes, scales = mx_tiles[half_batch, chunks.start]
            res = psum.tile([P, HALF, DIM], F32, tag="bank")
            for i in range(len(chunks)):
                tokens = slice(i * P, (i + 1) * P)
                nc.tensor.matmul_mx(
                    out=res[:, i, :],
                    lhsT=codes[:, tokens].bitcast(FP8X4),
                    lhsT_scale=scales[:, tokens],
                    rhs=wp_codes[:].bitcast(FP8X4),
                    rhs_scale=wp_scales[:],
                    start=True,
                    stop=True,
                )
            res_tiles[half_batch, chunks.start] = res

        def store(half_batch, chunks, out_sb):
            b, half = divmod(half_batch, 2)
            first = half * HALF + chunks.start
            out_by_token = out[b].rearrange("(p c) n -> p c n", c=CHUNKS)
            nc.sync.dma_start(out=out_by_token[:, first : first + len(chunks), :], in_=out_sb[:, 0 : len(chunks), :])

        def finish_on_gpsimd(half_batch):
            res_sb = res_pool.tile([P, HALF, DIM], F32)
            nc.scalar.copy(out=res_sb[:], in_=res_tiles[half_batch, 0][:])
            out_sb = out_pool.tile([P, HALF, DIM], F32)
            nc.gpsimd.tensor_tensor(out=out_sb[:], in0=res_sb[:], in1=bias_for(HALF), op=ADD)
            store(half_batch, range(HALF), out_sb)

        def finish_on_vector(half_batch, chunks):
            n = len(chunks)
            out_sb = out_pool.tile([P, HALF, DIM], F32)
            nc.vector.tensor_tensor(
                out=out_sb[:, 0:n, :], in0=res_tiles[half_batch, chunks.start][:, 0:n, :], in1=bias_for(n), op=ADD
            )
            store(half_batch, chunks, out_sb)

        def queries_due(r):
            return range(1 if r == 0 else r + TRANSPOSE_LEAD, min(r + TRANSPOSE_LEAD + 1, PAIRS))

        def inverses_due(r):
            if r == 0:
                return range(1, PAIRS_PER_HALF)
            if (r + 1) % PAIRS_PER_HALF == 0 and r + 1 < PAIRS:
                return range(r + 1, r + 1 + PAIRS_PER_HALF)
            return range(0)

        def run_round(r):
            stage_round = PAIRS if r == PAIRS - 1 else r
            quantise_due = half_batch_due(stage_round, QUANTISE_LAG)
            project_due = half_batch_due(stage_round, PROJECT_LAG)

            queries = [(pair, cc, h) for pair in queries_due(r) for cc in range(PAIR) for h in range(H)]
            woven = 0
            for cc in range(PAIR):
                for h in range(H):
                    multiply(r, cc, h)
                    if (cc, h) == (0, H - 1):
                        if project_due is not None:
                            project(project_due, range(HALF))
                    elif woven < len(queries):
                        transpose_query(*queries[woven])
                        woven += 1
            for query in queries[woven:]:
                transpose_query(*query)
            if r == 0:
                for pair in queries_due(r):
                    keep_queries(pair, range(PAIR))
            if len(inverses_due(r)) > 0:
                denominators(inverses_due(r))
            if r >= OM_LAG:
                transpose_outputs(r - OM_LAG, range(PAIR))

            if quantise_due is not None:
                quantise(quantise_due, range(HALF))
            for cc in range(PAIR):
                for h in range(H):
                    if (cc, h) == (0, H - 2) and is_wide(r, PAIR - 1, 0):
                        invert_wide(r)
                    if not is_shared(r, cc, h):
                        normalise(r, cc, h)
            if len(inverses_due(r)) > 0:
                invert(inverses_due(r))

            if is_shared(r, PAIR - 1, H - 1):
                normalise_shared(r, PAIR - 1, H - 1)
            if project_due is not None and r < PAIRS - 1:
                finish_on_gpsimd(project_due)
            if r > 0:
                for pair in queries_due(r):
                    keep_queries(pair, range(PAIR))
            if r >= OM_LAG:
                regroup(r - OM_LAG, range(PAIR))

        for cc in range(PAIR):
            for h in range(H):
                transpose_query(0, cc, h)
            keep_queries(0, range(cc, cc + 1))
        turn_k_sum()
        denominators(range(0, 1))
        invert(range(0, 1))

        for r in range(PAIRS):
            run_round(r)
            if r == SPLIT_ROUND:
                split_weights()
            if r == TURN_ROUND - 1:
                spread_bias()
            if r == TURN_ROUND:
                turn_weights()
            if r == WEIGHTS_ROUND:
                quantise_weights()

        last = HALVES - 1
        finish_on_vector(last - 2, range(HALF))
        project(last - 1, range(HALF))
        for cc in range(PAIR):
            transpose_outputs(PAIRS - 1, range(cc, cc + 1))
            regroup(PAIRS - 1, range(cc, cc + 1))
        parts = [range(0, PAIR)] + [range(c, c + 1) for c in range(PAIR, HALF)]
        for part in parts:
            quantise(last, part)
            project(last, part)
            if part.start == 0:
                finish_on_vector(last - 1, range(HALF))
        for part in parts:
            finish_on_vector(last, part)
